import numpy as np
import ml_dtypes


def mxq(x, axis, fmt="e4m3"):
    dtype, down = {"e4m3": (ml_dtypes.float8_e4m3fn, 7), "e5m2": (ml_dtypes.float8_e5m2, 14)}[fmt]
    v = np.moveaxis(np.asarray(x, np.float32).astype(ml_dtypes.bfloat16).astype(np.float64), axis, -1)
    blocks = v.reshape(v.shape[:-1] + (-1, 32))
    amax = np.abs(blocks).max(-1, keepdims=True)
    byte = np.maximum(np.where(amax > 0, np.frexp(amax)[1] - 1 + 127, 0) - down, 1)
    scale = np.exp2(byte - 127.0)
    codes = (blocks / scale).astype(np.float32).astype(dtype).astype(np.float64)
    return np.moveaxis((codes * scale).reshape(v.shape), -1, axis)


WIDE = False


def mx_kscale(k):
    if not WIDE:
        return np.ones(k)
    levels = np.array([10, -10, 5, -5, 0])
    a = np.random.permutation(np.resize(levels, k // 512 * 4)).reshape(k // 512, 4)
    idx = np.arange(k)
    return np.exp2(a[idx // 512, idx % 128 // 32])


BF16 = ml_dtypes.bfloat16


def bf(x):
    return np.asarray(x, np.float32).astype(BF16)


def f64(x):
    return np.asarray(x).astype(np.float64)


P, N, Z, H1, H2, C = 2, 4096, 16, 512, 1024, 512
EPS = 1e-5


def batch_norm(h, gamma, beta):
    mu = h.mean(axis=1, keepdims=True)
    var = h.var(axis=1, keepdims=True)
    return (h - mu) * (1.0 / np.sqrt(var + EPS)) * gamma[:, None, :] + beta[:, None, :]


def setup_inputs():
    r = np.random.standard_normal
    t = mx_kscale(H2)
    sd = np.where(np.random.random((P, 1, H2)) < 0.25, np.sqrt(EPS), 1.0)
    return {"h7_pre": bf((r((P, N, H2)) + 0.5 * r((P, 1, H2))) * sd),
            "g7": bf((1.0 + 0.1 * r((P, H2))) * t),
            "be7": bf(0.3 * r((P, H2)) * t),
            "W8": bf(1.5 * r((P, C, H2)) / np.sqrt(H2) / t),
            "b8": bf(0.5 * r((P, C)))}


def reference(h7_pre, g7, be7, W8, b8):
    a = np.maximum(batch_norm(f64(h7_pre), f64(g7), f64(be7)), 0.0)
    y = (mxq(a, 2, "e4m3") @ mxq(f64(W8), 2, "e4m3").transpose(0, 2, 1)) + f64(b8)[:, None, :]
    em = 1.0 / (1.0 + np.exp(-y))
    return em.transpose(1, 0, 2)

@@ -1,0 +1,340 @@
+from contextlib import ExitStack
+
+import concourse.mybir as mybir
+from concourse.masks import make_identity
+
+F32 = mybir.dt.float32
+BF16 = mybir.dt.bfloat16
+U32 = mybir.dt.uint32
+U8 = mybir.dt.uint8
+FP8X4 = mybir.dt.float8_e4m3fn_x4
+ALU = mybir.AluOpType
+ACT = mybir.ActivationFunctionType
+AX = mybir.AxisListType
+
+P = 128
+NB = 2
+N = 4096
+K = 1024
+C = 512
+EPS = 1e-5
+NJ = N // P
+KT = K // P
+NH = 8
+NBN = 2
+XBUFS = 5
+PRE = 2
+FLOPS = 2 * NB * N * K * C
+
+
+def tile_decoder_pb_t_kernel(tc, h7_pre, g7, be7, W8, b8, out):
+    nc = tc.nc
+    with ExitStack() as ctx:
+        ctx.enter_context(tc.manual_schedule())
+        keep = ctx.enter_context(tc.tile_pool(name="keep", bufs=1))
+        xpool = ctx.enter_context(tc.tile_pool(name="xpool", bufs=XBUFS))
+        rtpool = ctx.enter_context(tc.tile_pool(name="rtpool", bufs=13))
+        gpool = ctx.enter_context(tc.tile_pool(name="gpool", bufs=3))
+        cpool = ctx.enter_context(tc.tile_pool(name="cpool", bufs=3))
+        ypool = ctx.enter_context(tc.tile_pool(name="ypool", bufs=3))
+        jpool = ctx.enter_context(tc.tile_pool(name="jpool", bufs=2))
+        tpool = ctx.enter_context(tc.psum_pool(name="tpool", bufs=3))
+        apool = ctx.enter_context(tc.psum_pool(name="apool", bufs=4))
+        spool = ctx.enter_context(tc.psum_pool(name="spool", bufs=1))
+
+        xv = [h7_pre[b].rearrange("(p j) k -> p j k", j=NJ) for b in range(NB)]
+        ov = [out[:, b, :].rearrange("(p j) c -> p j c", j=NJ) for b in range(NB)]
+
+        xt = {}
+        rt = {}
+        grp = {}
+        codes = {}
+        acc = {}
+        yt = {}
+        wn = {}
+        wc = {}
+        ws = {}
+        bias = {}
+        st = {}
+        state = {"ld": 0}
+
+        ident = keep.tile([P, P], BF16, name="ident")
+        make_identity(nc, ident[:])
+        ones = keep.tile([P, 2], BF16, name="ones")
+        nc.vector.memset(ones[:], 1.0)
+        mhalf = keep.tile([P, KT], F32, name="mhalf")
+        nc.vector.memset(mhalf[:], -0.5)
+        warm = keep.tile([P, 1], F32, name="warm")
+        nc.vector.memset(warm[:], 0.0)
+        nc.scalar.activation(out=warm[:], in_=warm[:], func=ACT.Sigmoid)
+        gbrows = keep.tile([P, P], BF16, name="gbrows")
+        nc.vector.memset(gbrows[:], 0.0)
+        gb = keep.tile([P, 4 * KT], F32, name="gb")
+        sums = spool.tile([P, NB * NJ * KT], F32, name="sums")
+
+        def load_w(b):
+            wn[b] = rtpool.tile([P, 4, K], BF16, name="wn", tag="rt", align_bytes=64)
+            nc.sync.dma_start(out=wn[b][:], in_=W8[b].rearrange("(a p) k -> p a k", p=P))
+
+        def load_small():
+            nc.sync.dma_start(out=gbrows[0:16, :], in_=g7.rearrange("b (t p) -> (b t) p", p=P))
+            nc.sync.dma_start(out=gbrows[16:32, :], in_=be7.rearrange("b (t p) -> (b t) p", p=P))
+            for b in range(NB):
+                bias[b] = keep.tile([P, C], BF16, name="bias%d" % b)
+                nc.sync.dma_start(out=bias[b][:], in_=b8[b].partition_broadcast(P))
+
+        def load_x():
+            a = state["ld"]
+            if a < NB * NH:
+                xt[a] = xpool.tile([P, 4, K], BF16, name="xt")
+                nc.sync.dma_start(out=xt[a][:], in_=xv[a // NH][:, 4 * (a % NH) : 4 * (a % NH) + 4, :])
+                state["ld"] = a + 1
+                if a == 2:
+                    load_small()
+
+        def prep_w(b):
+            gw = rtpool.tile([P, 2, C, 4], BF16, name="gw", tag="rt", align_bytes=64)
+            for g in range(2):
+                for hc in range(2):
+                    tp = tpool.tile([P, 1024], BF16, name="tp")
+                    for t in range(4):
+                        for a in range(2):
+                            nc.tensor.transpose(
+                                tp[:, t * 256 + a * P : t * 256 + (a + 1) * P],
+                                wn[b][:, 2 * hc + a, (4 * g + t) * P : (4 * g + t + 1) * P],
+                                ident[:],
+                            )
+                    dst = gw[:, g, hc * 256 : (hc + 1) * 256, :]
+                    src = tp[:].rearrange("p (t c) -> p c t", t=4)
+                    if hc == 0:
+                        nc.vector.tensor_copy(out=dst, in_=src)
+                    else:
+                        nc.scalar.copy(out=dst, in_=src)
+            wc[b] = keep.tile([P, 2, C], U32, name="wc%d" % b, align_bytes=64)
+            ws[b] = keep.tile([P, 2, C], U8, name="ws%d" % b, align_bytes=64)
+            nc.vector.quantize_mx(
+                out=wc[b][:].rearrange("p g c -> p (g c)").bitcast(FP8X4),
+                scales=ws[b][:].rearrange("p g c -> p (g c)"),
+                in_=gw[:].rearrange("p g c t -> p (g c t)"),
+            )
+
+        def prep_gb():
+            tp = tpool.tile([P, 1024], BF16, name="tp")
+            nc.tensor.transpose(tp[:, 0:P], gbrows[:], ident[:])
+            nc.vector.tensor_copy(out=gb[:], in_=tp[:, 0 : 4 * KT])
+
+        def a_half(a):
+            b = a // NH
+            h = a % NH
+            x = xt[a]
+            r = rtpool.tile([P, KT, 512], BF16, name="rt", tag="rt", align_bytes=64)
+            rt[a] = r
+            if h == 0:
+                st[b] = {
+                    "sq": keep.tile([P, KT, NH], F32, name="sq%d" % b),
+                    "bst": keep.tile([P, NBN, NH, 6], F32, name="bst%d" % b),
+                    "cpiv": keep.tile([P, KT], F32, name="cpiv%d" % b),
+                }
+            s = st[b]
+            for q in range(4):
+                tp = tpool.tile([P, 1024], BF16, name="tp")
+                for k2 in range(2):
+                    for jj in range(4):
+                        nc.tensor.transpose(
+                            tp[:, k2 * 512 + jj * P : k2 * 512 + (jj + 1) * P],
+                            x[:, jj, (2 * q + k2) * P : (2 * q + k2 + 1) * P],
+                            ident[:],
+                        )
+                dst = r[:, 2 * q : 2 * q + 2, :]
+                src = tp[:].rearrange("p (k n) -> p k n", k=2)
+                if a < NH + PRE:
+                    nc.vector.tensor_copy(out=dst, in_=src)
+                else:
+                    nc.scalar.copy(out=dst, in_=src)
+            for jj in range(4):
+                for kt in range(NBN, KT):
+                    col = (b * NJ + 4 * h + jj) * KT + kt
+                    nc.tensor.matmul(
+                        out=sums[:, col : col + 1],
+                        lhsT=x[:, jj, kt * P : (kt + 1) * P],
+                        rhs=ones[:, 0:1],
+                        start=True,
+                        stop=True,
+                    )
+            load_x()
+            if h == 0:
+                nc.vector.tensor_copy(out=s["cpiv"][:], in_=r[:, :, 0])
+            for kt in range(KT):
+                if kt < NBN:
+                    nc.vector.bn_stats(out=s["bst"][:, kt, h, :], in_=r[:, kt, :])
+                else:
+                    junk = jpool.tile([P, 512], BF16, name="junk")
+                    nc.scalar.activation(
+                        out=junk[:],
+                        in_=r[:, kt, :],
+                        func=ACT.Square,
+                        bias=s["cpiv"][:, kt : kt + 1],
+                        scale=-1.0,
+                        accum_out=s["sq"][:, kt, h : h + 1],
+                    )
+
+        def fin_mean(b):
+            s = st[b]
+            for nm in ("sumx", "mean", "dd", "d2", "ssq", "var", "ve", "rstd", "sc", "ms", "sh"):
+                s[nm] = keep.tile([P, KT], F32, name="%s%d" % (nm, b))
+            s["mv"] = keep.tile([P, NBN, 2], F32, name="mv%d" % b)
+            lo = slice(NBN, KT)
+            nc.vector.tensor_reduce(
+                out=s["sumx"][:, lo],
+                in_=sums[:, b * NJ * KT : (b + 1) * NJ * KT].rearrange("p (j t) -> p t j", t=KT)[:, lo, :],
+                axis=AX.X,
+                op=ALU.add,
+            )
+            nc.vector.tensor_scalar(out=s["mean"][:, lo], in0=s["sumx"][:, lo], scalar1=1.0 / N, scalar2=None, op0=ALU.mult)
+            nc.vector.tensor_tensor(out=s["dd"][:, lo], in0=s["cpiv"][:, lo], in1=s["mean"][:, lo], op=ALU.subtract)
+            nc.vector.tensor_tensor(out=s["d2"][:, lo], in0=s["dd"][:, lo], in1=s["dd"][:, lo], op=ALU.mult)
+            for kt in range(NBN):
+                nc.vector.bn_aggr(out=s["mv"][:, kt, :], in_=s["bst"][:, kt].rearrange("p h s -> p (h s)"))
+            nc.vector.tensor_copy(out=s["mean"][:, 0:NBN], in_=s["mv"][:, :, 0])
+            nc.vector.tensor_copy(out=s["var"][:, 0:NBN], in_=s["mv"][:, :, 1])
+
+        def fin_a(b):
+            s = st[b]
+            lo = slice(NBN, KT)
+            nc.vector.tensor_reduce(out=s["ssq"][:, lo], in_=s["sq"][:, lo, :], axis=AX.X, op=ALU.add)
+            nc.vector.scalar_tensor_tensor(
+                out=s["var"][:, lo], in0=s["ssq"][:, lo], scalar=1.0 / N, in1=s["d2"][:, lo], op0=ALU.mult, op1=ALU.subtract
+            )
+            nc.vector.tensor_scalar(out=s["ve"][:], in0=s["var"][:], scalar1=0.0, scalar2=EPS, op0=ALU.max, op1=ALU.add)
+            nc.gpsimd.tensor_tensor(out=s["rstd"][:], in0=s["ve"][:], in1=mhalf[:], op=ALU.pow)
+
+        def fin_b(b):
+            s = st[b]
+            nc.vector.tensor_tensor(out=s["sc"][:], in0=gb[:, b * KT : (b + 1) * KT], in1=s["rstd"][:], op=ALU.mult)
+            nc.vector.tensor_tensor(out=s["ms"][:], in0=s["mean"][:], in1=s["sc"][:], op=ALU.mult)
+            nc.vector.tensor_tensor(out=s["sh"][:], in0=gb[:, (2 + b) * KT : (3 + b) * KT], in1=s["ms"][:], op=ALU.subtract)
+
+        def d1(w):
+            s = st[w // NH]
+            r = rt[w]
+            for kt in range(KT):
+                nc.vector.tensor_scalar(
+                    out=r[:, kt, :],
+                    in0=r[:, kt, :],
+                    scalar1=s["sc"][:, kt : kt + 1],
+                    scalar2=s["sh"][:, kt : kt + 1],
+                    op0=ALU.mult,
+                    op1=ALU.add,
+                )
+
+        def d2(w, g, on_scalar):
+            if w not in grp:
+                grp[w] = gpool.tile([P, 2, 512, 4], BF16, name="grp", align_bytes=64)
+            dst = grp[w][:, g].rearrange("p (c i) t -> p c t i", i=4)
+            src = rt[w][:, 4 * g : 4 * g + 4, :].rearrange("p t (c i) -> p c t i", i=4)
+            if on_scalar:
+                nc.scalar.activation(out=dst, in_=src, func=ACT.Relu)
+            else:
+                nc.vector.tensor_scalar(out=dst, in0=src, scalar1=0.0, scalar2=None, op0=ALU.max)
+
+        def quant(w):
+            ac = cpool.tile([P, 2, 512], U32, name="ac", align_bytes=64)
+            asc = cpool.tile([P, 2, 512], U8, name="asc", align_bytes=64)
+            codes[w] = (ac, asc)
+            nc.vector.quantize_mx(
+                out=ac[:].rearrange("p g c -> p (g c)").bitcast(FP8X4),
+                scales=asc[:].rearrange("p g c -> p (g c)"),
+                in_=grp[w][:].rearrange("p g c t -> p (g c t)"),
+            )
+
+        def mx(w, jj):
+            b = w // NH
+            ac, asc = codes[w]
+            t = apool.tile([P, C], F32, name="acc")
+            acc[(w, jj)] = t
+            for g in range(2):
+                nc.tensor.matmul_mx(
+                    out=t[:],
+                    lhsT=ac[:, g, jj * P : (jj + 1) * P].bitcast(FP8X4),
+                    lhsT_scale=asc[:, g, jj * P : (jj + 1) * P],
+                    rhs=wc[b][:, g, :].bitcast(FP8X4),
+                    rhs_scale=ws[b][:, g, :],
+                    start=(g == 0),
+                    stop=(g == 1),
+                )
+
+        def addb(w, jj):
+            if jj == 0:
+                yt[w] = ypool.tile([P, 4, C], F32, name="y")
+            nc.vector.tensor_tensor(out=yt[w][:, jj, :], in0=acc[(w, jj)][:], in1=bias[w // NH][:], op=ALU.add)
+
+        def sigm(w, j0, j1):
+            nc.scalar.activation(out=yt[w][:, j0:j1, :], in_=yt[w][:, j0:j1, :], func=ACT.Sigmoid)
+
+        def store(w, j0, j1):
+            u = w % NH
+            nc.scalar.dma_start(out=ov[w // NH][:, 4 * u + j0 : 4 * u + j1, :], in_=yt[w][:, j0:j1, :])
+
+        def deep(w):
+            return (2 <= w < NH) or w >= NH + 2
+
+        def s_takes(w, g):
+            return w >= NH + 2 and g == 1
+
+        load_w(0)
+        load_w(1)
+        for i in range(XBUFS):
+            load_x()
+        prep_w(0)
+        prep_w(1)
+        for a in range(NH):
+            a_half(a)
+            if a == 4:
+                prep_gb()
+        fin_mean(0)
+        for a in range(NH, NH + PRE):
+            a_half(a)
+        fin_a(0)
+        fin_b(0)
+        d1(0)
+        d2(0, 0, False)
+        d2(0, 1, False)
+        d1(1)
+        nxt = NH + PRE
+        for w in range(2 * NH):
+            quant(w)
+            if w + 2 < 2 * NH and deep(w + 2):
+                d1(w + 2)
+            if w == NH - 1:
+                fin_mean(1)
+                fin_a(1)
+            for jj in range(4):
+                if w > 0:
+                    addb(w - 1, jj)
+                mx(w, jj)
+                if w > 0 and jj % 2 == 1:
+                    sigm(w - 1, jj - 1, jj + 1)
+            if w > 0:
+                store(w - 1, 0, 4)
+            if w == NH - 1:
+                fin_b(1)
+                d1(NH)
+            if w == NH:
+                d1(NH + 1)
+            if w + 2 < 2 * NH and deep(w + 2):
+                for g in range(2):
+                    if s_takes(w + 2, g):
+                        d2(w + 2, g, True)
+            if w + 1 < 2 * NH:
+                for g in range(2):
+                    if not (deep(w + 1) and s_takes(w + 1, g)):
+                        d2(w + 1, g, False)
+            if nxt < 2 * NH:
+                a_half(nxt)
+                nxt += 1
+        last = 2 * NH - 1
+        for jj in range(4):
+            addb(last, jj)
+            sigm(last, jj, jj + 1)
+            if jj % 2 == 1:
+                store(last, jj - 1, jj + 1)

@@ -21,9 +21,11 @@ EPS = 1e-5
 NJ = N // P
 KT = K // P
 NH = 8
-NBN = 2
+NG = (2, 3)
+NV = (2, 0)
 XBUFS = 5
 PRE = 2
+SUMCOL = 384
 FLOPS = 2 * NB * N * K * C
 
 
@@ -38,6 +40,7 @@ def tile_decoder_pb_t_kernel(tc, h7_pre, g7, be7, W8, b8, out):
         cpool = ctx.enter_context(tc.tile_pool(name="cpool", bufs=3))
         ypool = ctx.enter_context(tc.tile_pool(name="ypool", bufs=3))
         jpool = ctx.enter_context(tc.tile_pool(name="jpool", bufs=2))
+        dpool = ctx.enter_context(tc.tile_pool(name="dpool", bufs=2))
         tpool = ctx.enter_context(tc.psum_pool(name="tpool", bufs=3))
         apool = ctx.enter_context(tc.psum_pool(name="apool", bufs=4))
         spool = ctx.enter_context(tc.psum_pool(name="spool", bufs=1))
@@ -52,6 +55,7 @@ def tile_decoder_pb_t_kernel(tc, h7_pre, g7, be7, W8, b8, out):
         acc = {}
         yt = {}
         wn = {}
+        gws = {}
         wc = {}
         ws = {}
         bias = {}
@@ -70,7 +74,7 @@ def tile_decoder_pb_t_kernel(tc, h7_pre, g7, be7, W8, b8, out):
         gbrows = keep.tile([P, P], BF16, name="gbrows")
         nc.vector.memset(gbrows[:], 0.0)
         gb = keep.tile([P, 4 * KT], F32, name="gb")
-        sums = spool.tile([P, NB * NJ * KT], F32, name="sums")
+        stt = spool.tile([P, 512], F32, name="stt")
 
         def load_w(b):
             wn[b] = rtpool.tile([P, 4, K], BF16, name="wn", tag="rt", align_bytes=64)
@@ -90,10 +94,15 @@ def tile_decoder_pb_t_kernel(tc, h7_pre, g7, be7, W8, b8, out):
                 nc.sync.dma_start(out=xt[a][:], in_=xv[a // NH][:, 4 * (a % NH) : 4 * (a % NH) + 4, :])
                 state["ld"] = a + 1
                 if a == 2:
+                    load_w(0)
+                if a == 5:
                     load_small()
+                if a == 8:
+                    load_w(1)
 
-        def prep_w(b):
+        def w_tr(b):
             gw = rtpool.tile([P, 2, C, 4], BF16, name="gw", tag="rt", align_bytes=64)
+            gws[b] = gw
             for g in range(2):
                 for hc in range(2):
                     tp = tpool.tile([P, 1024], BF16, name="tp")
@@ -106,10 +115,10 @@ def tile_decoder_pb_t_kernel(tc, h7_pre, g7, be7, W8, b8, out):
                             )
                     dst = gw[:, g, hc * 256 : (hc + 1) * 256, :]
                     src = tp[:].rearrange("p (t c) -> p c t", t=4)
-                    if hc == 0:
-                        nc.vector.tensor_copy(out=dst, in_=src)
-                    else:
-                        nc.scalar.copy(out=dst, in_=src)
+                    nc.scalar.copy(out=dst, in_=src)
+
+        def w_q(b):
+            gw = gws[b]
             wc[b] = keep.tile([P, 2, C], U32, name="wc%d" % b, align_bytes=64)
             ws[b] = keep.tile([P, 2, C], U8, name="ws%d" % b, align_bytes=64)
             nc.vector.quantize_mx(
@@ -126,16 +135,34 @@ def tile_decoder_pb_t_kernel(tc, h7_pre, g7, be7, W8, b8, out):
         def a_half(a):
             b = a // NH
             h = a % NH
+            ng = NG[b]
+            nb = KT - NV[b]
             x = xt[a]
             r = rtpool.tile([P, KT, 512], BF16, name="rt", tag="rt", align_bytes=64)
             rt[a] = r
             if h == 0:
                 st[b] = {
                     "sq": keep.tile([P, KT, NH], F32, name="sq%d" % b),
-                    "bst": keep.tile([P, NBN, NH, 6], F32, name="bst%d" % b),
                     "cpiv": keep.tile([P, KT], F32, name="cpiv%d" % b),
                 }
+                if NV[b] > 0:
+                    st[b]["bst"] = keep.tile([P, NV[b], NH, 6], F32, name="bst%d" % b)
+                nc.vector.memset(st[b]["cpiv"][:], 0.0)
             s = st[b]
+
+            def gram():
+                for i in range(ng):
+                    for jj in range(4):
+                        nc.tensor.matmul(
+                            out=stt[:, i * P : (i + 1) * P],
+                            lhsT=x[:, jj, i * P : (i + 1) * P],
+                            rhs=x[:, jj, i * P : (i + 1) * P],
+                            start=(h == 0 and i == 0 and jj == 0),
+                            stop=False,
+                        )
+
+            if a != NH:
+                gram()
             for q in range(4):
                 tp = tpool.tile([P, 1024], BF16, name="tp")
                 for k2 in range(2):
@@ -147,26 +174,27 @@ def tile_decoder_pb_t_kernel(tc, h7_pre, g7, be7, W8, b8, out):
                         )
                 dst = r[:, 2 * q : 2 * q + 2, :]
                 src = tp[:].rearrange("p (k n) -> p k n", k=2)
-                if a < NH + PRE:
+                if a <= NH:
                     nc.vector.tensor_copy(out=dst, in_=src)
                 else:
                     nc.scalar.copy(out=dst, in_=src)
+            if a == NH:
+                gram()
             for jj in range(4):
-                for kt in range(NBN, KT):
-                    col = (b * NJ + 4 * h + jj) * KT + kt
+                for kt in range(nb):
                     nc.tensor.matmul(
-                        out=sums[:, col : col + 1],
+                        out=stt[:, SUMCOL + kt : SUMCOL + kt + 1],
                         lhsT=x[:, jj, kt * P : (kt + 1) * P],
                         rhs=ones[:, 0:1],
-                        start=True,
-                        stop=True,
+                        start=False,
+                        stop=(h == NH - 1 and jj == 3 and kt == nb - 1),
                     )
             load_x()
             if h == 0:
-                nc.vector.tensor_copy(out=s["cpiv"][:], in_=r[:, :, 0])
-            for kt in range(KT):
-                if kt < NBN:
-                    nc.vector.bn_stats(out=s["bst"][:, kt, h, :], in_=r[:, kt, :])
+                nc.vector.tensor_copy(out=s["cpiv"][:, ng:nb], in_=r[:, ng:nb, 0])
+            for kt in range(ng, KT):
+                if kt >= nb:
+                    nc.vector.bn_stats(out=s["bst"][:, kt - nb, h, :], in_=r[:, kt, :])
                 else:
                     junk = jpool.tile([P, 512], BF16, name="junk")
                     nc.scalar.activation(
@@ -180,30 +208,34 @@ def tile_decoder_pb_t_kernel(tc, h7_pre, g7, be7, W8, b8, out):
 
         def fin_mean(b):
             s = st[b]
-            for nm in ("sumx", "mean", "dd", "d2", "ssq", "var", "ve", "rstd", "sc", "ms", "sh"):
+            ng = NG[b]
+            nv = NV[b]
+            nb = KT - nv
+            for nm in ("mean", "dd", "d2", "ssq", "var", "ve", "rstd", "sc", "ms", "sh"):
                 s[nm] = keep.tile([P, KT], F32, name="%s%d" % (nm, b))
-            s["mv"] = keep.tile([P, NBN, 2], F32, name="mv%d" % b)
-            lo = slice(NBN, KT)
-            nc.vector.tensor_reduce(
-                out=s["sumx"][:, lo],
-                in_=sums[:, b * NJ * KT : (b + 1) * NJ * KT].rearrange("p (j t) -> p t j", t=KT)[:, lo, :],
-                axis=AX.X,
-                op=ALU.add,
+            nc.vector.tensor_scalar(
+                out=s["mean"][:, 0:nb], in0=stt[:, SUMCOL : SUMCOL + nb], scalar1=1.0 / N, scalar2=None, op0=ALU.mult
             )
-            nc.vector.tensor_scalar(out=s["mean"][:, lo], in0=s["sumx"][:, lo], scalar1=1.0 / N, scalar2=None, op0=ALU.mult)
-            nc.vector.tensor_tensor(out=s["dd"][:, lo], in0=s["cpiv"][:, lo], in1=s["mean"][:, lo], op=ALU.subtract)
-            nc.vector.tensor_tensor(out=s["d2"][:, lo], in0=s["dd"][:, lo], in1=s["dd"][:, lo], op=ALU.mult)
-            for kt in range(NBN):
-                nc.vector.bn_aggr(out=s["mv"][:, kt, :], in_=s["bst"][:, kt].rearrange("p h s -> p (h s)"))
-            nc.vector.tensor_copy(out=s["mean"][:, 0:NBN], in_=s["mv"][:, :, 0])
-            nc.vector.tensor_copy(out=s["var"][:, 0:NBN], in_=s["mv"][:, :, 1])
+            for i in range(ng):
+                dg = dpool.tile([P, P], F32, name="dg")
+                nc.vector.tensor_tensor(out=dg[:], in0=stt[:, i * P : (i + 1) * P], in1=ident[:], op=ALU.mult)
+                nc.vector.tensor_reduce(out=s["ssq"][:, i : i + 1], in_=dg[:], axis=AX.X, op=ALU.add)
+            nc.vector.tensor_tensor(out=s["dd"][:, 0:nb], in0=s["cpiv"][:, 0:nb], in1=s["mean"][:, 0:nb], op=ALU.subtract)
+            nc.vector.tensor_tensor(out=s["d2"][:, 0:nb], in0=s["dd"][:, 0:nb], in1=s["dd"][:, 0:nb], op=ALU.mult)
+            if nv > 0:
+                s["mv"] = keep.tile([P, nv, 2], F32, name="mv%d" % b)
+                for i in range(nv):
+                    nc.vector.bn_aggr(out=s["mv"][:, i, :], in_=s["bst"][:, i].rearrange("p h s -> p (h s)"))
+                nc.vector.tensor_copy(out=s["mean"][:, nb:KT], in_=s["mv"][:, :, 0])
+                nc.vector.tensor_copy(out=s["var"][:, nb:KT], in_=s["mv"][:, :, 1])
 
         def fin_a(b):
             s = st[b]
-            lo = slice(NBN, KT)
-            nc.vector.tensor_reduce(out=s["ssq"][:, lo], in_=s["sq"][:, lo, :], axis=AX.X, op=ALU.add)
+            ng = NG[b]
+            nb = KT - NV[b]
+            nc.vector.tensor_reduce(out=s["ssq"][:, ng:nb], in_=s["sq"][:, ng:nb, :], axis=AX.X, op=ALU.add)
             nc.vector.scalar_tensor_tensor(
-                out=s["var"][:, lo], in0=s["ssq"][:, lo], scalar=1.0 / N, in1=s["d2"][:, lo], op0=ALU.mult, op1=ALU.subtract
+                out=s["var"][:, 0:nb], in0=s["ssq"][:, 0:nb], scalar=1.0 / N, in1=s["d2"][:, 0:nb], op0=ALU.mult, op1=ALU.subtract
             )
             nc.vector.tensor_scalar(out=s["ve"][:], in0=s["var"][:], scalar1=0.0, scalar2=EPS, op0=ALU.max, op1=ALU.add)
             nc.gpsimd.tensor_tensor(out=s["rstd"][:], in0=s["ve"][:], in1=mhalf[:], op=ALU.pow)
@@ -281,25 +313,24 @@ def tile_decoder_pb_t_kernel(tc, h7_pre, g7, be7, W8, b8, out):
         def s_takes(w, g):
             return w >= NH + 2 and g == 1
 
-        load_w(0)
-        load_w(1)
         for i in range(XBUFS):
             load_x()
-        prep_w(0)
-        prep_w(1)
         for a in range(NH):
             a_half(a)
             if a == 4:
-                prep_gb()
+                w_tr(0)
+            if a == 5:
+                w_q(0)
+        prep_gb()
         fin_mean(0)
-        for a in range(NH, NH + PRE):
-            a_half(a)
         fin_a(0)
+        a_half(NH)
         fin_b(0)
         d1(0)
         d2(0, 0, False)
         d2(0, 1, False)
         d1(1)
+        a_half(NH + 1)
         nxt = NH + PRE
         for w in range(2 * NH):
             quant(w)
@@ -329,6 +360,10 @@ def tile_decoder_pb_t_kernel(tc, h7_pre, g7, be7, W8, b8, out):
                 for g in range(2):
                     if not (deep(w + 1) and s_takes(w + 1, g)):
                         d2(w + 1, g, False)
+            if w == 2:
+                w_tr(1)
+            if w == 4:
+                w_q(1)
             if nxt < 2 * NH:
                 a_half(nxt)
                 nxt += 1

@@ -80,9 +80,11 @@ def tile_decoder_pb_t_kernel(tc, h7_pre, g7, be7, W8, b8, out):
             wn[b] = rtpool.tile([P, 4, K], BF16, name="wn", tag="rt", align_bytes=64)
             nc.sync.dma_start(out=wn[b][:], in_=W8[b].rearrange("(a p) k -> p a k", p=P))
 
-        def load_small():
+        def load_gb():
             nc.sync.dma_start(out=gbrows[0:16, :], in_=g7.rearrange("b (t p) -> (b t) p", p=P))
             nc.sync.dma_start(out=gbrows[16:32, :], in_=be7.rearrange("b (t p) -> (b t) p", p=P))
+
+        def load_bias():
             for b in range(NB):
                 bias[b] = keep.tile([P, C], BF16, name="bias%d" % b)
                 nc.sync.dma_start(out=bias[b][:], in_=b8[b].partition_broadcast(P))
@@ -93,11 +95,12 @@ def tile_decoder_pb_t_kernel(tc, h7_pre, g7, be7, W8, b8, out):
                 xt[a] = xpool.tile([P, 4, K], BF16, name="xt")
                 nc.sync.dma_start(out=xt[a][:], in_=xv[a // NH][:, 4 * (a % NH) : 4 * (a % NH) + 4, :])
                 state["ld"] = a + 1
-                if a == 2:
+                if a == 7:
+                    load_gb()
                     load_w(0)
-                if a == 5:
-                    load_small()
-                if a == 8:
+                if a == 9:
+                    load_bias()
+                if a == 11:
                     load_w(1)
 
         def w_tr(b):
@@ -174,7 +177,7 @@ def tile_decoder_pb_t_kernel(tc, h7_pre, g7, be7, W8, b8, out):
                         )
                 dst = r[:, 2 * q : 2 * q + 2, :]
                 src = tp[:].rearrange("p (k n) -> p k n", k=2)
-                if a <= NH:
+                if a < NH or (a > NH and q == 0):
                     nc.vector.tensor_copy(out=dst, in_=src)
                 else:
                     nc.scalar.copy(out=dst, in_=src)
@@ -311,25 +314,23 @@ def tile_decoder_pb_t_kernel(tc, h7_pre, g7, be7, W8, b8, out):
             return (2 <= w < NH) or w >= NH + 2
 
         def s_takes(w, g):
-            return w >= NH + 2 and g == 1
+            return w >= NH + 2 and (g == 1 or w % 2 == 0)
 
         for i in range(XBUFS):
             load_x()
         for a in range(NH):
             a_half(a)
-            if a == 4:
-                w_tr(0)
-            if a == 5:
-                w_q(0)
         prep_gb()
+        w_tr(0)
         fin_mean(0)
         fin_a(0)
-        a_half(NH)
         fin_b(0)
         d1(0)
         d2(0, 0, False)
         d2(0, 1, False)
+        w_q(0)
         d1(1)
+        a_half(NH)
         a_half(NH + 1)
         nxt = NH + PRE
         for w in range(2 * NH):
@@ -360,9 +361,9 @@ def tile_decoder_pb_t_kernel(tc, h7_pre, g7, be7, W8, b8, out):
                 for g in range(2):
                     if not (deep(w + 1) and s_takes(w + 1, g)):
                         d2(w + 1, g, False)
-            if w == 2:
+            if w == 6:
                 w_tr(1)
-            if w == 4:
+            if w == 7:
                 w_q(1)
             if nxt < 2 * NH:
                 a_half(nxt)

@@ -314,7 +314,7 @@ def tile_decoder_pb_t_kernel(tc, h7_pre, g7, be7, W8, b8, out):
             return (2 <= w < NH) or w >= NH + 2
 
         def s_takes(w, g):
-            return w >= NH + 2 and (g == 1 or w % 2 == 0)
+            return w >= NH + 2 and g == 1
 
         for i in range(XBUFS):
             load_x()

@@ -25,6 +25,7 @@ NG = (2, 3)
 NV = (2, 0)
 XBUFS = 5
 PRE = 2
+EARLY = 2
 SUMCOL = 384
 FLOPS = 2 * NB * N * K * C
 
@@ -49,6 +50,7 @@ def tile_decoder_pb_t_kernel(tc, h7_pre, g7, be7, W8, b8, out):
         ov = [out[:, b, :].rearrange("(p j) c -> p j c", j=NJ) for b in range(NB)]
 
         xt = {}
+        tps = {}
         rt = {}
         grp = {}
         codes = {}
@@ -135,7 +137,38 @@ def tile_decoder_pb_t_kernel(tc, h7_pre, g7, be7, W8, b8, out):
             nc.tensor.transpose(tp[:, 0:P], gbrows[:], ident[:])
             nc.vector.tensor_copy(out=gb[:], in_=tp[:, 0 : 4 * KT])
 
-        def a_half(a):
+        def gram(a):
+            b = a // NH
+            h = a % NH
+            x = xt[a]
+            for i in range(NG[b]):
+                for jj in range(4):
+                    nc.tensor.matmul(
+                        out=stt[:, i * P : (i + 1) * P],
+                        lhsT=x[:, jj, i * P : (i + 1) * P],
+                        rhs=x[:, jj, i * P : (i + 1) * P],
+                        start=(h == 0 and i == 0 and jj == 0),
+                        stop=False,
+                    )
+
+        def flip(a, q):
+            x = xt[a]
+            tp = tpool.tile([P, 1024], BF16, name="tp")
+            tps[(a, q)] = tp
+            for k2 in range(2):
+                for jj in range(4):
+                    nc.tensor.transpose(
+                        tp[:, k2 * 512 + jj * P : k2 * 512 + (jj + 1) * P],
+                        x[:, jj, (2 * q + k2) * P : (2 * q + k2 + 1) * P],
+                        ident[:],
+                    )
+
+        def a_begin(a):
+            gram(a)
+            for q in range(EARLY):
+                flip(a, q)
+
+        def a_half(a, begun):
             b = a // NH
             h = a % NH
             ng = NG[b]
@@ -152,37 +185,19 @@ def tile_decoder_pb_t_kernel(tc, h7_pre, g7, be7, W8, b8, out):
                     st[b]["bst"] = keep.tile([P, NV[b], NH, 6], F32, name="bst%d" % b)
                 nc.vector.memset(st[b]["cpiv"][:], 0.0)
             s = st[b]
-
-            def gram():
-                for i in range(ng):
-                    for jj in range(4):
-                        nc.tensor.matmul(
-                            out=stt[:, i * P : (i + 1) * P],
-                            lhsT=x[:, jj, i * P : (i + 1) * P],
-                            rhs=x[:, jj, i * P : (i + 1) * P],
-                            start=(h == 0 and i == 0 and jj == 0),
-                            stop=False,
-                        )
-
-            if a != NH:
-                gram()
+            if a != NH and not begun:
+                gram(a)
             for q in range(4):
-                tp = tpool.tile([P, 1024], BF16, name="tp")
-                for k2 in range(2):
-                    for jj in range(4):
-                        nc.tensor.transpose(
-                            tp[:, k2 * 512 + jj * P : k2 * 512 + (jj + 1) * P],
-                            x[:, jj, (2 * q + k2) * P : (2 * q + k2 + 1) * P],
-                            ident[:],
-                        )
+                if not (begun and q < EARLY):
+                    flip(a, q)
                 dst = r[:, 2 * q : 2 * q + 2, :]
-                src = tp[:].rearrange("p (k n) -> p k n", k=2)
-                if a < NH or (a > NH and q == 0):
+                src = tps[(a, q)][:].rearrange("p (k n) -> p k n", k=2)
+                if a < NH or (a > NH and q < EARLY):
                     nc.vector.tensor_copy(out=dst, in_=src)
                 else:
                     nc.scalar.copy(out=dst, in_=src)
             if a == NH:
-                gram()
+                gram(a)
             for jj in range(4):
                 for kt in range(nb):
                     nc.tensor.matmul(
@@ -314,12 +329,12 @@ def tile_decoder_pb_t_kernel(tc, h7_pre, g7, be7, W8, b8, out):
             return (2 <= w < NH) or w >= NH + 2
 
         def s_takes(w, g):
-            return w >= NH + 2 and g == 1
+            return w >= NH + 2 and (g == 1 or w % 2 == 0)
 
         for i in range(XBUFS):
             load_x()
         for a in range(NH):
-            a_half(a)
+            a_half(a, False)
         prep_gb()
         w_tr(0)
         fin_mean(0)
@@ -330,10 +345,12 @@ def tile_decoder_pb_t_kernel(tc, h7_pre, g7, be7, W8, b8, out):
         d2(0, 1, False)
         w_q(0)
         d1(1)
-        a_half(NH)
-        a_half(NH + 1)
+        a_half(NH, False)
+        a_half(NH + 1, False)
         nxt = NH + PRE
         for w in range(2 * NH):
+            if nxt < 2 * NH:
+                a_begin(nxt)
             quant(w)
             if w + 2 < 2 * NH and deep(w + 2):
                 d1(w + 2)
@@ -366,7 +383,7 @@ def tile_decoder_pb_t_kernel(tc, h7_pre, g7, be7, W8, b8, out):
             if w == 7:
                 w_q(1)
             if nxt < 2 * NH:
-                a_half(nxt)
+                a_half(nxt, True)
                 nxt += 1
         last = 2 * NH - 1
         for jj in range(4):

@@ -192,7 +192,7 @@ def tile_decoder_pb_t_kernel(tc, h7_pre, g7, be7, W8, b8, out):
                     flip(a, q)
                 dst = r[:, 2 * q : 2 * q + 2, :]
                 src = tps[(a, q)][:].rearrange("p (k n) -> p k n", k=2)
-                if a < NH or (a > NH and q < EARLY):
+                if a < NH:
                     nc.vector.tensor_copy(out=dst, in_=src)
                 else:
                     nc.scalar.copy(out=dst, in_=src)

@@ -21,8 +21,8 @@ EPS = 1e-5
 NJ = N // P
 KT = K // P
 NH = 8
-NG = (2, 3)
-NV = (2, 0)
+NG = (3, 3)
+NV = (0, 0)
 XBUFS = 5
 PRE = 2
 EARLY = 2
@@ -148,7 +148,7 @@ def tile_decoder_pb_t_kernel(tc, h7_pre, g7, be7, W8, b8, out):
                         lhsT=x[:, jj, i * P : (i + 1) * P],
                         rhs=x[:, jj, i * P : (i + 1) * P],
                         start=(h == 0 and i == 0 and jj == 0),
-                        stop=False,
+                        stop=(b == 0 and h == NH - 1 and i == NG[b] - 1 and jj == 3),
                     )
 
         def flip(a, q):
@@ -181,6 +181,8 @@ def tile_decoder_pb_t_kernel(tc, h7_pre, g7, be7, W8, b8, out):
                     "sq": keep.tile([P, KT, NH], F32, name="sq%d" % b),
                     "cpiv": keep.tile([P, KT], F32, name="cpiv%d" % b),
                 }
+                if b == 0:
+                    st[b]["sm"] = keep.tile([P, KT, NH], F32, name="sm%d" % b)
                 if NV[b] > 0:
                     st[b]["bst"] = keep.tile([P, NV[b], NH, 6], F32, name="bst%d" % b)
                 nc.vector.memset(st[b]["cpiv"][:], 0.0)
@@ -193,12 +195,21 @@ def tile_decoder_pb_t_kernel(tc, h7_pre, g7, be7, W8, b8, out):
                 dst = r[:, 2 * q : 2 * q + 2, :]
                 src = tps[(a, q)][:].rearrange("p (k n) -> p k n", k=2)
                 if a < NH:
-                    nc.vector.tensor_copy(out=dst, in_=src)
+                    for k2 in range(2):
+                        nc.vector.tensor_scalar(
+                            out=r[:, 2 * q + k2, :],
+                            in0=tps[(a, q)][:, k2 * 512 : (k2 + 1) * 512],
+                            scalar1=1.0,
+                            scalar2=0.0,
+                            op0=ALU.mult,
+                            op1=ALU.add,
+                            accum_out=s["sm"][:, 2 * q + k2, h : h + 1],
+                        )
                 else:
                     nc.scalar.copy(out=dst, in_=src)
             if a == NH:
                 gram(a)
-            for jj in range(4):
+            for jj in range(4 if b == 1 else 0):
                 for kt in range(nb):
                     nc.tensor.matmul(
                         out=stt[:, SUMCOL + kt : SUMCOL + kt + 1],
@@ -231,9 +242,14 @@ def tile_decoder_pb_t_kernel(tc, h7_pre, g7, be7, W8, b8, out):
             nb = KT - nv
             for nm in ("mean", "dd", "d2", "ssq", "var", "ve", "rstd", "sc", "ms", "sh"):
                 s[nm] = keep.tile([P, KT], F32, name="%s%d" % (nm, b))
-            nc.vector.tensor_scalar(
-                out=s["mean"][:, 0:nb], in0=stt[:, SUMCOL : SUMCOL + nb], scalar1=1.0 / N, scalar2=None, op0=ALU.mult
-            )
+            if b == 0:
+                s["tot"] = keep.tile([P, KT], F32, name="tot%d" % b)
+                nc.vector.tensor_reduce(out=s["tot"][:], in_=s["sm"][:], axis=AX.X, op=ALU.add)
+                nc.vector.tensor_scalar(out=s["mean"][:], in0=s["tot"][:], scalar1=1.0 / N, scalar2=None, op0=ALU.mult)
+            else:
+                nc.vector.tensor_scalar(
+                    out=s["mean"][:, 0:nb], in0=stt[:, SUMCOL : SUMCOL + nb], scalar1=1.0 / N, scalar2=None, op0=ALU.mult
+                )
             for i in range(ng):
                 dg = dpool.tile([P, P], F32, name="dg")
                 nc.vector.tensor_tensor(out=dg[:], in0=stt[:, i * P : (i + 1) * P], in1=ident[:], op=ALU.mult)

@@ -25,6 +25,8 @@ NG = (3, 3)
 NV = (0, 0)
 XBUFS = 5
 PRE = 2
+VQ = 1
+BF16_MAX = 3.3895313892515355e38
 EARLY = 2
 SUMCOL = 384
 FLOPS = 2 * NB * N * K * C
@@ -168,14 +170,22 @@ def tile_decoder_pb_t_kernel(tc, h7_pre, g7, be7, W8, b8, out):
             for q in range(EARLY):
                 flip(a, q)
 
+        def a_vcopy(a):
+            rt[a] = rtpool.tile([P, KT, 512], BF16, name="rt", tag="rt", align_bytes=64)
+            for q in range(VQ):
+                nc.vector.tensor_copy(
+                    out=rt[a][:, 2 * q : 2 * q + 2, :], in_=tps[(a, q)][:].rearrange("p (k n) -> p k n", k=2)
+                )
+
         def a_half(a, begun):
             b = a // NH
             h = a % NH
             ng = NG[b]
             nb = KT - NV[b]
             x = xt[a]
-            r = rtpool.tile([P, KT, 512], BF16, name="rt", tag="rt", align_bytes=64)
-            rt[a] = r
+            if a not in rt:
+                rt[a] = rtpool.tile([P, KT, 512], BF16, name="rt", tag="rt", align_bytes=64)
+            r = rt[a]
             if h == 0:
                 st[b] = {
                     "sq": keep.tile([P, KT, NH], F32, name="sq%d" % b),
@@ -205,6 +215,10 @@ def tile_decoder_pb_t_kernel(tc, h7_pre, g7, be7, W8, b8, out):
                             op1=ALU.add,
                             accum_out=s["sm"][:, 2 * q + k2, h : h + 1],
                         )
+                elif begun and q < VQ:
+                    pass
+                elif a > NH and q < VQ:
+                    nc.vector.tensor_copy(out=dst, in_=src)
                 else:
                     nc.scalar.copy(out=dst, in_=src)
             if a == NH:
@@ -293,12 +307,22 @@ def tile_decoder_pb_t_kernel(tc, h7_pre, g7, be7, W8, b8, out):
                     op1=ALU.add,
                 )
 
-        def d2(w, g, on_scalar):
+        def d2(w, g, eng):
             if w not in grp:
                 grp[w] = gpool.tile([P, 2, 512, 4], BF16, name="grp", align_bytes=64)
+            if eng == "G":
+                nc.gpsimd.tensor_scalar(
+                    out=grp[w][:, g],
+                    in0=rt[w][:, 4 * g : 4 * g + 4, :].rearrange("p t c -> p c t"),
+                    scalar1=BF16_MAX,
+                    scalar2=0.0,
+                    op0=ALU.min,
+                    op1=ALU.max,
+                )
+                return
             dst = grp[w][:, g].rearrange("p (c i) t -> p c t i", i=4)
             src = rt[w][:, 4 * g : 4 * g + 4, :].rearrange("p t (c i) -> p c t i", i=4)
-            if on_scalar:
+            if eng == "S":
                 nc.scalar.activation(out=dst, in_=src, func=ACT.Relu)
             else:
                 nc.vector.tensor_scalar(out=dst, in0=src, scalar1=0.0, scalar2=None, op0=ALU.max)
@@ -344,8 +368,12 @@ def tile_decoder_pb_t_kernel(tc, h7_pre, g7, be7, W8, b8, out):
         def deep(w):
             return (2 <= w < NH) or w >= NH + 2
 
-        def s_takes(w, g):
-            return w >= NH + 2 and (g == 1 or w % 2 == 0)
+        def who(w, g):
+            if not deep(w):
+                return "V"
+            if g == 0:
+                return "G"
+            return "V" if w < NH else "S"
 
         for i in range(XBUFS):
             load_x()
@@ -357,8 +385,8 @@ def tile_decoder_pb_t_kernel(tc, h7_pre, g7, be7, W8, b8, out):
         fin_a(0)
         fin_b(0)
         d1(0)
-        d2(0, 0, False)
-        d2(0, 1, False)
+        d2(0, 0, "V")
+        d2(0, 1, "V")
         w_q(0)
         d1(1)
         a_half(NH, False)
@@ -370,6 +398,7 @@ def tile_decoder_pb_t_kernel(tc, h7_pre, g7, be7, W8, b8, out):
             quant(w)
             if w + 2 < 2 * NH and deep(w + 2):
                 d1(w + 2)
+                d2(w + 2, 0, "G")
             if w == NH - 1:
                 fin_mean(1)
                 fin_a(1)
@@ -388,12 +417,14 @@ def tile_decoder_pb_t_kernel(tc, h7_pre, g7, be7, W8, b8, out):
                 d1(NH + 1)
             if w + 2 < 2 * NH and deep(w + 2):
                 for g in range(2):
-                    if s_takes(w + 2, g):
-                        d2(w + 2, g, True)
+                    if who(w + 2, g) == "S":
+                        d2(w + 2, g, "S")
+            if nxt < 2 * NH:
+                a_vcopy(nxt)
             if w + 1 < 2 * NH:
                 for g in range(2):
-                    if not (deep(w + 1) and s_takes(w + 1, g)):
-                        d2(w + 1, g, False)
+                    if who(w + 1, g) == "V":
+                        d2(w + 1, g, "V")
             if w == 6:
                 w_tr(1)
             if w == 7:

@@ -21,14 +21,13 @@ EPS = 1e-5
 NJ = N // P
 KT = K // P
 NH = 8
-NG = (3, 3)
-NV = (0, 0)
-XBUFS = 5
+NU = NB * NH
+NG = 3
+NS = KT - NG
 PRE = 2
-VQ = 1
-BF16_MAX = 3.3895313892515355e38
-EARLY = 2
 SUMCOL = 384
+NV2 = 7
+BF16_MAX = 3.3895313892515355e38
 FLOPS = 2 * NB * N * K * C
 
 
@@ -37,8 +36,8 @@ def tile_decoder_pb_t_kernel(tc, h7_pre, g7, be7, W8, b8, out):
     with ExitStack() as ctx:
         ctx.enter_context(tc.manual_schedule())
         keep = ctx.enter_context(tc.tile_pool(name="keep", bufs=1))
-        xpool = ctx.enter_context(tc.tile_pool(name="xpool", bufs=XBUFS))
-        rtpool = ctx.enter_context(tc.tile_pool(name="rtpool", bufs=13))
+        xpool = ctx.enter_context(tc.tile_pool(name="xpool", bufs=NH))
+        rtpool = ctx.enter_context(tc.tile_pool(name="rtpool", bufs=11))
         gpool = ctx.enter_context(tc.tile_pool(name="gpool", bufs=3))
         cpool = ctx.enter_context(tc.tile_pool(name="cpool", bufs=3))
         ypool = ctx.enter_context(tc.tile_pool(name="ypool", bufs=3))
@@ -79,6 +78,13 @@ def tile_decoder_pb_t_kernel(tc, h7_pre, g7, be7, W8, b8, out):
         nc.vector.memset(gbrows[:], 0.0)
         gb = keep.tile([P, 4 * KT], F32, name="gb")
         stt = spool.tile([P, 512], F32, name="stt")
+        for b in range(NB):
+            st[b] = {
+                "sq": keep.tile([P, NS, NH], F32, name="sq%d" % b),
+                "cpiv": keep.tile([P, KT], F32, name="cpiv%d" % b),
+            }
+            nc.vector.memset(st[b]["cpiv"][:], 0.0)
+        st[0]["sm"] = keep.tile([P, KT, NH], F32, name="sm0")
 
         def load_w(b):
             wn[b] = rtpool.tile([P, 4, K], BF16, name="wn", tag="rt", align_bytes=64)
@@ -95,9 +101,14 @@ def tile_decoder_pb_t_kernel(tc, h7_pre, g7, be7, W8, b8, out):
 
         def load_x():
             a = state["ld"]
-            if a < NB * NH:
+            if a < NU:
                 xt[a] = xpool.tile([P, 4, K], BF16, name="xt")
-                nc.sync.dma_start(out=xt[a][:], in_=xv[a // NH][:, 4 * (a % NH) : 4 * (a % NH) + 4, :])
+                src = xv[a // NH][:, 4 * (a % NH) : 4 * (a % NH) + 4, :]
+                if a == 0:
+                    for q in range(4):
+                        nc.sync.dma_start(out=xt[a][:, :, 256 * q : 256 * (q + 1)], in_=src[:, :, 256 * q : 256 * (q + 1)])
+                else:
+                    nc.sync.dma_start(out=xt[a][:], in_=src)
                 state["ld"] = a + 1
                 if a == 7:
                     load_gb()
@@ -107,22 +118,23 @@ def tile_decoder_pb_t_kernel(tc, h7_pre, g7, be7, W8, b8, out):
                 if a == 11:
                     load_w(1)
 
-        def w_tr(b):
-            gw = rtpool.tile([P, 2, C, 4], BF16, name="gw", tag="rt", align_bytes=64)
-            gws[b] = gw
-            for g in range(2):
-                for hc in range(2):
-                    tp = tpool.tile([P, 1024], BF16, name="tp")
-                    for t in range(4):
-                        for a in range(2):
-                            nc.tensor.transpose(
-                                tp[:, t * 256 + a * P : t * 256 + (a + 1) * P],
-                                wn[b][:, 2 * hc + a, (4 * g + t) * P : (4 * g + t + 1) * P],
-                                ident[:],
-                            )
-                    dst = gw[:, g, hc * 256 : (hc + 1) * 256, :]
-                    src = tp[:].rearrange("p (t c) -> p c t", t=4)
-                    nc.scalar.copy(out=dst, in_=src)
+        def w_tr(b, part):
+            if part == 0:
+                gws[b] = rtpool.tile([P, 2, C, 4], BF16, name="gw", tag="rt", align_bytes=64)
+            gw = gws[b]
+            g = part // 2
+            hc = part % 2
+            tp = tpool.tile([P, 1024], BF16, name="tp")
+            for t in range(4):
+                for a in range(2):
+                    nc.tensor.transpose(
+                        tp[:, t * 256 + a * P : t * 256 + (a + 1) * P],
+                        wn[b][:, 2 * hc + a, (4 * g + t) * P : (4 * g + t + 1) * P],
+                        ident[:],
+                    )
+            dst = gw[:, g, hc * 256 : (hc + 1) * 256, :]
+            src = tp[:].rearrange("p (t c) -> p c t", t=4)
+            nc.scalar.copy(out=dst, in_=src)
 
         def w_q(b):
             gw = gws[b]
@@ -143,21 +155,34 @@ def tile_decoder_pb_t_kernel(tc, h7_pre, g7, be7, W8, b8, out):
             b = a // NH
             h = a % NH
             x = xt[a]
-            for i in range(NG[b]):
+            for i in range(NG):
                 for jj in range(4):
                     nc.tensor.matmul(
                         out=stt[:, i * P : (i + 1) * P],
-                        lhsT=x[:, jj, i * P : (i + 1) * P],
-                        rhs=x[:, jj, i * P : (i + 1) * P],
+                        lhsT=x[:, jj, (NS + i) * P : (NS + i + 1) * P],
+                        rhs=x[:, jj, (NS + i) * P : (NS + i + 1) * P],
                         start=(h == 0 and i == 0 and jj == 0),
-                        stop=(b == 0 and h == NH - 1 and i == NG[b] - 1 and jj == 3),
+                        stop=(b == 0 and h == NH - 1 and i == NG - 1 and jj == 3),
                     )
 
-        def flip(a, q):
+        def sums(a):
+            h = a % NH
+            x = xt[a]
+            for jj in range(4):
+                for kt in range(KT):
+                    nc.tensor.matmul(
+                        out=stt[:, SUMCOL + kt : SUMCOL + kt + 1],
+                        lhsT=x[:, jj, kt * P : (kt + 1) * P],
+                        rhs=ones[:, 0:1],
+                        start=False,
+                        stop=(h == NH - 1 and jj == 3 and kt == KT - 1),
+                    )
+
+        def flip(a, q, nk=2):
             x = xt[a]
             tp = tpool.tile([P, 1024], BF16, name="tp")
             tps[(a, q)] = tp
-            for k2 in range(2):
+            for k2 in range(nk):
                 for jj in range(4):
                     nc.tensor.transpose(
                         tp[:, k2 * 512 + jj * P : k2 * 512 + (jj + 1) * P],
@@ -165,95 +190,62 @@ def tile_decoder_pb_t_kernel(tc, h7_pre, g7, be7, W8, b8, out):
                         ident[:],
                     )
 
-        def a_begin(a):
-            gram(a)
-            for q in range(EARLY):
-                flip(a, q)
+        def square(a, kt, src):
+            s = st[a // NH]
+            junk = jpool.tile([P, 512], BF16, name="junk")
+            nc.scalar.activation(
+                out=junk[:],
+                in_=src,
+                func=ACT.Square,
+                bias=s["cpiv"][:, kt : kt + 1],
+                scale=-1.0,
+                accum_out=s["sq"][:, kt, a % NH : a % NH + 1],
+            )
 
-        def a_vcopy(a):
-            rt[a] = rtpool.tile([P, KT, 512], BF16, name="rt", tag="rt", align_bytes=64)
-            for q in range(VQ):
-                nc.vector.tensor_copy(
-                    out=rt[a][:, 2 * q : 2 * q + 2, :], in_=tps[(a, q)][:].rearrange("p (k n) -> p k n", k=2)
-                )
-
-        def a_half(a, begun):
-            b = a // NH
-            h = a % NH
-            ng = NG[b]
-            nb = KT - NV[b]
-            x = xt[a]
-            if a not in rt:
-                rt[a] = rtpool.tile([P, KT, 512], BF16, name="rt", tag="rt", align_bytes=64)
-            r = rt[a]
-            if h == 0:
-                st[b] = {
-                    "sq": keep.tile([P, KT, NH], F32, name="sq%d" % b),
-                    "cpiv": keep.tile([P, KT], F32, name="cpiv%d" % b),
-                }
-                if b == 0:
-                    st[b]["sm"] = keep.tile([P, KT, NH], F32, name="sm%d" % b)
-                if NV[b] > 0:
-                    st[b]["bst"] = keep.tile([P, NV[b], NH, 6], F32, name="bst%d" % b)
-                nc.vector.memset(st[b]["cpiv"][:], 0.0)
-            s = st[b]
-            if a != NH and not begun:
-                gram(a)
+        def p1_head(a):
+            s = st[0]
+            r = rtpool.tile([P, KT, 512], BF16, name="rt", tag="rt", align_bytes=64)
+            rt[a] = r
             for q in range(4):
-                if not (begun and q < EARLY):
-                    flip(a, q)
-                dst = r[:, 2 * q : 2 * q + 2, :]
-                src = tps[(a, q)][:].rearrange("p (k n) -> p k n", k=2)
-                if a < NH:
-                    for k2 in range(2):
-                        nc.vector.tensor_scalar(
-                            out=r[:, 2 * q + k2, :],
-                            in0=tps[(a, q)][:, k2 * 512 : (k2 + 1) * 512],
-                            scalar1=1.0,
-                            scalar2=0.0,
-                            op0=ALU.mult,
-                            op1=ALU.add,
-                            accum_out=s["sm"][:, 2 * q + k2, h : h + 1],
-                        )
-                elif begun and q < VQ:
-                    pass
-                elif a > NH and q < VQ:
-                    nc.vector.tensor_copy(out=dst, in_=src)
-                else:
-                    nc.scalar.copy(out=dst, in_=src)
-            if a == NH:
-                gram(a)
-            for jj in range(4 if b == 1 else 0):
-                for kt in range(nb):
-                    nc.tensor.matmul(
-                        out=stt[:, SUMCOL + kt : SUMCOL + kt + 1],
-                        lhsT=x[:, jj, kt * P : (kt + 1) * P],
-                        rhs=ones[:, 0:1],
-                        start=False,
-                        stop=(h == NH - 1 and jj == 3 and kt == nb - 1),
+                if q == 3:
+                    gram(a)
+                flip(a, q)
+                for k2 in range(2):
+                    nc.vector.tensor_scalar(
+                        out=r[:, 2 * q + k2, :],
+                        in0=tps[(a, q)][:, k2 * 512 : (k2 + 1) * 512],
+                        scalar1=1.0,
+                        scalar2=0.0,
+                        op0=ALU.mult,
+                        op1=ALU.add,
+                        accum_out=s["sm"][:, 2 * q + k2, a : a + 1],
                     )
+                if a == 0 and q == 2:
+                    nc.vector.tensor_copy(out=s["cpiv"][:, 0:NS], in_=r[:, 0:NS, 0])
             load_x()
-            if h == 0:
-                nc.vector.tensor_copy(out=s["cpiv"][:, ng:nb], in_=r[:, ng:nb, 0])
-            for kt in range(ng, KT):
-                if kt >= nb:
-                    nc.vector.bn_stats(out=s["bst"][:, kt - nb, h, :], in_=r[:, kt, :])
-                else:
-                    junk = jpool.tile([P, 512], BF16, name="junk")
-                    nc.scalar.activation(
-                        out=junk[:],
-                        in_=r[:, kt, :],
-                        func=ACT.Square,
-                        bias=s["cpiv"][:, kt : kt + 1],
-                        scale=-1.0,
-                        accum_out=s["sq"][:, kt, h : h + 1],
+            for kt in range(NS):
+                square(a, kt, r[:, kt, :])
+
+        def p1(a):
+            s = st[1]
+            flip(a, 0)
+            flip(a, 1)
+            flip(a, 2, 1)
+            gram(a)
+            sums(a)
+            for q in range(3):
+                if a == NH:
+                    nk = 2 if q < 2 else 1
+                    nc.scalar.copy(
+                        out=s["cpiv"][:, 2 * q : 2 * q + nk],
+                        in_=tps[(a, q)][:].rearrange("p (k n) -> p k n", k=2)[:, 0:nk, 0],
                     )
+            for kt in range(NS):
+                square(a, kt, tps[(a, kt // 2)][:, (kt % 2) * 512 : (kt % 2 + 1) * 512])
+            load_x()
 
         def fin_mean(b):
             s = st[b]
-            ng = NG[b]
-            nv = NV[b]
-            nb = KT - nv
             for nm in ("mean", "dd", "d2", "ssq", "var", "ve", "rstd", "sc", "ms", "sh"):
                 s[nm] = keep.tile([P, KT], F32, name="%s%d" % (nm, b))
             if b == 0:
@@ -262,28 +254,20 @@ def tile_decoder_pb_t_kernel(tc, h7_pre, g7, be7, W8, b8, out):
                 nc.vector.tensor_scalar(out=s["mean"][:], in0=s["tot"][:], scalar1=1.0 / N, scalar2=None, op0=ALU.mult)
             else:
                 nc.vector.tensor_scalar(
-                    out=s["mean"][:, 0:nb], in0=stt[:, SUMCOL : SUMCOL + nb], scalar1=1.0 / N, scalar2=None, op0=ALU.mult
+                    out=s["mean"][:], in0=stt[:, SUMCOL : SUMCOL + KT], scalar1=1.0 / N, scalar2=None, op0=ALU.mult
                 )
-            for i in range(ng):
+            for i in range(NG):
                 dg = dpool.tile([P, P], F32, name="dg")
                 nc.vector.tensor_tensor(out=dg[:], in0=stt[:, i * P : (i + 1) * P], in1=ident[:], op=ALU.mult)
-                nc.vector.tensor_reduce(out=s["ssq"][:, i : i + 1], in_=dg[:], axis=AX.X, op=ALU.add)
-            nc.vector.tensor_tensor(out=s["dd"][:, 0:nb], in0=s["cpiv"][:, 0:nb], in1=s["mean"][:, 0:nb], op=ALU.subtract)
-            nc.vector.tensor_tensor(out=s["d2"][:, 0:nb], in0=s["dd"][:, 0:nb], in1=s["dd"][:, 0:nb], op=ALU.mult)
-            if nv > 0:
-                s["mv"] = keep.tile([P, nv, 2], F32, name="mv%d" % b)
-                for i in range(nv):
-                    nc.vector.bn_aggr(out=s["mv"][:, i, :], in_=s["bst"][:, i].rearrange("p h s -> p (h s)"))
-                nc.vector.tensor_copy(out=s["mean"][:, nb:KT], in_=s["mv"][:, :, 0])
-                nc.vector.tensor_copy(out=s["var"][:, nb:KT], in_=s["mv"][:, :, 1])
+                nc.vector.tensor_reduce(out=s["ssq"][:, NS + i : NS + i + 1], in_=dg[:], axis=AX.X, op=ALU.add)
+            nc.vector.tensor_tensor(out=s["dd"][:], in0=s["cpiv"][:], in1=s["mean"][:], op=ALU.subtract)
+            nc.vector.tensor_tensor(out=s["d2"][:], in0=s["dd"][:], in1=s["dd"][:], op=ALU.mult)
 
         def fin_a(b):
             s = st[b]
-            ng = NG[b]
-            nb = KT - NV[b]
-            nc.vector.tensor_reduce(out=s["ssq"][:, ng:nb], in_=s["sq"][:, ng:nb, :], axis=AX.X, op=ALU.add)
+            nc.vector.tensor_reduce(out=s["ssq"][:, 0:NS], in_=s["sq"][:], axis=AX.X, op=ALU.add)
             nc.vector.scalar_tensor_tensor(
-                out=s["var"][:, 0:nb], in0=s["ssq"][:, 0:nb], scalar=1.0 / N, in1=s["d2"][:, 0:nb], op0=ALU.mult, op1=ALU.subtract
+                out=s["var"][:], in0=s["ssq"][:], scalar=1.0 / N, in1=s["d2"][:], op0=ALU.mult, op1=ALU.subtract
             )
             nc.vector.tensor_scalar(out=s["ve"][:], in0=s["var"][:], scalar1=0.0, scalar2=EPS, op0=ALU.max, op1=ALU.add)
             nc.gpsimd.tensor_tensor(out=s["rstd"][:], in0=s["ve"][:], in1=mhalf[:], op=ALU.pow)
@@ -305,6 +289,23 @@ def tile_decoder_pb_t_kernel(tc, h7_pre, g7, be7, W8, b8, out):
                     scalar2=s["sh"][:, kt : kt + 1],
                     op0=ALU.mult,
                     op1=ALU.add,
+                )
+
+        def n2(w, kt):
+            s = st[1]
+            src = tps[(w, kt // 2)][:, (kt % 2) * 512 : (kt % 2 + 1) * 512]
+            if kt < NV2:
+                nc.vector.tensor_scalar(
+                    out=rt[w][:, kt, :],
+                    in0=src,
+                    scalar1=s["sc"][:, kt : kt + 1],
+                    scalar2=s["sh"][:, kt : kt + 1],
+                    op0=ALU.mult,
+                    op1=ALU.add,
+                )
+            else:
+                nc.scalar.activation(
+                    out=rt[w][:, kt, :], in_=src, func=ACT.Relu, bias=s["sh"][:, kt : kt + 1], scale=s["sc"][:, kt : kt + 1]
                 )
 
         def d2(w, g, eng):
@@ -365,22 +366,22 @@ def tile_decoder_pb_t_kernel(tc, h7_pre, g7, be7, W8, b8, out):
             u = w % NH
             nc.scalar.dma_start(out=ov[w // NH][:, 4 * u + j0 : 4 * u + j1, :], in_=yt[w][:, j0:j1, :])
 
-        def deep(w):
-            return (2 <= w < NH) or w >= NH + 2
-
         def who(w, g):
-            if not deep(w):
+            if w < 2:
                 return "V"
+            if w == 2:
+                return "S" if g == 0 else "V"
             if g == 0:
                 return "G"
             return "V" if w < NH else "S"
 
-        for i in range(XBUFS):
+        for i in range(NH):
             load_x()
         for a in range(NH):
-            a_half(a, False)
+            p1_head(a)
         prep_gb()
-        w_tr(0)
+        for part in range(4):
+            w_tr(0, part)
         fin_mean(0)
         fin_a(0)
         fin_b(0)
@@ -389,19 +390,34 @@ def tile_decoder_pb_t_kernel(tc, h7_pre, g7, be7, W8, b8, out):
         d2(0, 1, "V")
         w_q(0)
         d1(1)
-        a_half(NH, False)
-        a_half(NH + 1, False)
+        for a in range(NH, NH + PRE):
+            p1(a)
         nxt = NH + PRE
-        for w in range(2 * NH):
-            if nxt < 2 * NH:
-                a_begin(nxt)
+        for w in range(NU):
+            u = w + 2
+            if nxt < NU:
+                p1(nxt)
+                nxt += 1
+            elif u < NU:
+                for q in range(3):
+                    flip(u, q)
             quant(w)
-            if w + 2 < 2 * NH and deep(w + 2):
-                d1(w + 2)
-                d2(w + 2, 0, "G")
-            if w == NH - 1:
+            if w == NH - 2:
                 fin_mean(1)
                 fin_a(1)
+                fin_b(1)
+            if u < NH:
+                d1(u)
+                if who(u, 0) == "G":
+                    d2(u, 0, "G")
+            elif u < NU:
+                rt[u] = rtpool.tile([P, KT, 512], BF16, name="rt", tag="rt", align_bytes=64)
+                for kt in range(KT):
+                    if kt == 6:
+                        flip(u, 3)
+                    n2(u, kt)
+                    if kt == 3:
+                        d2(u, 0, "G")
             for jj in range(4):
                 if w > 0:
                     addb(w - 1, jj)
@@ -410,29 +426,19 @@ def tile_decoder_pb_t_kernel(tc, h7_pre, g7, be7, W8, b8, out):
                     sigm(w - 1, jj - 1, jj + 1)
             if w > 0:
                 store(w - 1, 0, 4)
-            if w == NH - 1:
-                fin_b(1)
-                d1(NH)
-            if w == NH:
-                d1(NH + 1)
-            if w + 2 < 2 * NH and deep(w + 2):
+            if u < NU:
                 for g in range(2):
-                    if who(w + 2, g) == "S":
-                        d2(w + 2, g, "S")
-            if nxt < 2 * NH:
-                a_vcopy(nxt)
-            if w + 1 < 2 * NH:
+                    if who(u, g) == "S":
+                        d2(u, g, "S")
+            if w + 1 < NU:
                 for g in range(2):
                     if who(w + 1, g) == "V":
                         d2(w + 1, g, "V")
-            if w == 6:
-                w_tr(1)
-            if w == 7:
+            if 1 <= w <= 4:
+                w_tr(1, w - 1)
+            if w == 5:
                 w_q(1)
-            if nxt < 2 * NH:
-                a_half(nxt, True)
-                nxt += 1
-        last = 2 * NH - 1
+        last = NU - 1
         for jj in range(4):
             addb(last, jj)
             sigm(last, jj, jj + 1)

@@ -26,7 +26,6 @@ NG = 3
 NS = KT - NG
 PRE = 2
 SUMCOL = 384
-NV2 = 7
 BF16_MAX = 3.3895313892515355e38
 FLOPS = 2 * NB * N * K * C
 
@@ -36,8 +35,8 @@ def tile_decoder_pb_t_kernel(tc, h7_pre, g7, be7, W8, b8, out):
     with ExitStack() as ctx:
         ctx.enter_context(tc.manual_schedule())
         keep = ctx.enter_context(tc.tile_pool(name="keep", bufs=1))
-        xpool = ctx.enter_context(tc.tile_pool(name="xpool", bufs=NH))
-        rtpool = ctx.enter_context(tc.tile_pool(name="rtpool", bufs=11))
+        xpool = ctx.enter_context(tc.tile_pool(name="xpool", bufs=5))
+        rtpool = ctx.enter_context(tc.tile_pool(name="rtpool", bufs=13))
         gpool = ctx.enter_context(tc.tile_pool(name="gpool", bufs=3))
         cpool = ctx.enter_context(tc.tile_pool(name="cpool", bufs=3))
         ypool = ctx.enter_context(tc.tile_pool(name="ypool", bufs=3))
@@ -226,23 +225,34 @@ def tile_decoder_pb_t_kernel(tc, h7_pre, g7, be7, W8, b8, out):
             for kt in range(NS):
                 square(a, kt, r[:, kt, :])
 
+        def bank_out(a, q, eng):
+            dst = rt[a][:, 2 * q : 2 * q + 2, :]
+            src = tps[(a, q)][:].rearrange("p (k n) -> p k n", k=2)
+            if eng == "V":
+                nc.vector.tensor_copy(out=dst, in_=src)
+            else:
+                nc.scalar.copy(out=dst, in_=src)
+
         def p1(a):
             s = st[1]
-            flip(a, 0)
-            flip(a, 1)
-            flip(a, 2, 1)
+            rt[a] = rtpool.tile([P, KT, 512], BF16, name="rt", tag="rt", align_bytes=64)
+            for q in range(3):
+                flip(a, q)
+            bank_out(a, 0, "S")
+            flip(a, 3)
             gram(a)
             sums(a)
-            for q in range(3):
-                if a == NH:
-                    nk = 2 if q < 2 else 1
-                    nc.scalar.copy(
-                        out=s["cpiv"][:, 2 * q : 2 * q + nk],
-                        in_=tps[(a, q)][:].rearrange("p (k n) -> p k n", k=2)[:, 0:nk, 0],
-                    )
-            for kt in range(NS):
-                square(a, kt, tps[(a, kt // 2)][:, (kt % 2) * 512 : (kt % 2 + 1) * 512])
+            bank_out(a, 1, "S")
+            nc.scalar.copy(out=rt[a][:, 4, :], in_=tps[(a, 2)][:, 0:512])
+            if a == NH:
+                nc.scalar.copy(out=s["cpiv"][:, 0:NS], in_=rt[a][:, 0:NS, 0])
             load_x()
+            for kt in range(NS):
+                square(a, kt, rt[a][:, kt, :])
+
+        def p1_v(a):
+            nc.vector.tensor_copy(out=rt[a][:, 5, :], in_=tps[(a, 2)][:, 512:1024])
+            bank_out(a, 3, "V")
 
         def fin_mean(b):
             s = st[b]
@@ -278,10 +288,10 @@ def tile_decoder_pb_t_kernel(tc, h7_pre, g7, be7, W8, b8, out):
             nc.vector.tensor_tensor(out=s["ms"][:], in0=s["mean"][:], in1=s["sc"][:], op=ALU.mult)
             nc.vector.tensor_tensor(out=s["sh"][:], in0=gb[:, (2 + b) * KT : (3 + b) * KT], in1=s["ms"][:], op=ALU.subtract)
 
-        def d1(w):
+        def d1(w, k0=0, k1=KT):
             s = st[w // NH]
             r = rt[w]
-            for kt in range(KT):
+            for kt in range(k0, k1):
                 nc.vector.tensor_scalar(
                     out=r[:, kt, :],
                     in0=r[:, kt, :],
@@ -289,23 +299,6 @@ def tile_decoder_pb_t_kernel(tc, h7_pre, g7, be7, W8, b8, out):
                     scalar2=s["sh"][:, kt : kt + 1],
                     op0=ALU.mult,
                     op1=ALU.add,
-                )
-
-        def n2(w, kt):
-            s = st[1]
-            src = tps[(w, kt // 2)][:, (kt % 2) * 512 : (kt % 2 + 1) * 512]
-            if kt < NV2:
-                nc.vector.tensor_scalar(
-                    out=rt[w][:, kt, :],
-                    in0=src,
-                    scalar1=s["sc"][:, kt : kt + 1],
-                    scalar2=s["sh"][:, kt : kt + 1],
-                    op0=ALU.mult,
-                    op1=ALU.add,
-                )
-            else:
-                nc.scalar.activation(
-                    out=rt[w][:, kt, :], in_=src, func=ACT.Relu, bias=s["sh"][:, kt : kt + 1], scale=s["sc"][:, kt : kt + 1]
                 )
 
         def d2(w, g, eng):
@@ -371,11 +364,15 @@ def tile_decoder_pb_t_kernel(tc, h7_pre, g7, be7, W8, b8, out):
                 return "V"
             if w == 2:
                 return "S" if g == 0 else "V"
+            if w == NH - 1:
+                return "G"
+            if w == NH:
+                return "S" if g == 0 else "V"
             if g == 0:
                 return "G"
-            return "V" if w < NH else "S"
+            return "V" if w <= NH + 1 else "S"
 
-        for i in range(NH):
+        for i in range(5):
             load_x()
         for a in range(NH):
             p1_head(a)
@@ -389,35 +386,26 @@ def tile_decoder_pb_t_kernel(tc, h7_pre, g7, be7, W8, b8, out):
         d2(0, 0, "V")
         d2(0, 1, "V")
         w_q(0)
+        p1(NH)
+        p1_v(NH)
         d1(1)
-        for a in range(NH, NH + PRE):
-            p1(a)
+        p1(NH + 1)
         nxt = NH + PRE
         for w in range(NU):
             u = w + 2
-            if nxt < NU:
-                p1(nxt)
-                nxt += 1
-            elif u < NU:
-                for q in range(3):
-                    flip(u, q)
             quant(w)
-            if w == NH - 2:
-                fin_mean(1)
-                fin_a(1)
-                fin_b(1)
-            if u < NH:
+            if w == NH:
+                w_q(1)
+            if u == NH - 1:
+                d1(u, 0, 4)
+                d2(u, 0, "G")
+            elif u == NH:
+                d1(u - 1, 4, KT)
+                d2(u - 1, 1, "G")
+            elif u < NU:
                 d1(u)
                 if who(u, 0) == "G":
                     d2(u, 0, "G")
-            elif u < NU:
-                rt[u] = rtpool.tile([P, KT, 512], BF16, name="rt", tag="rt", align_bytes=64)
-                for kt in range(KT):
-                    if kt == 6:
-                        flip(u, 3)
-                    n2(u, kt)
-                    if kt == 3:
-                        d2(u, 0, "G")
             for jj in range(4):
                 if w > 0:
                     addb(w - 1, jj)
@@ -426,6 +414,15 @@ def tile_decoder_pb_t_kernel(tc, h7_pre, g7, be7, W8, b8, out):
                     sigm(w - 1, jj - 1, jj + 1)
             if w > 0:
                 store(w - 1, 0, 4)
+            if nxt - 1 < NU and w <= NH - 2:
+                p1_v(nxt - 1)
+            if w == NH - 2:
+                for part in range(4):
+                    w_tr(1, part)
+                fin_mean(1)
+                fin_a(1)
+                fin_b(1)
+                d1(NH)
             if u < NU:
                 for g in range(2):
                     if who(u, g) == "S":
@@ -434,10 +431,9 @@ def tile_decoder_pb_t_kernel(tc, h7_pre, g7, be7, W8, b8, out):
                 for g in range(2):
                     if who(w + 1, g) == "V":
                         d2(w + 1, g, "V")
-            if 1 <= w <= 4:
-                w_tr(1, w - 1)
-            if w == 5:
-                w_q(1)
+            if nxt < NU:
+                p1(nxt)
+            nxt += 1
         last = NU - 1
         for jj in range(4):
             addb(last, jj)

@@ -268,8 +268,15 @@ def tile_decoder_pb_t_kernel(tc, h7_pre, g7, be7, W8, b8, out):
                 )
             for i in range(NG):
                 dg = dpool.tile([P, P], F32, name="dg")
-                nc.vector.tensor_tensor(out=dg[:], in0=stt[:, i * P : (i + 1) * P], in1=ident[:], op=ALU.mult)
-                nc.vector.tensor_reduce(out=s["ssq"][:, NS + i : NS + i + 1], in_=dg[:], axis=AX.X, op=ALU.add)
+                nc.vector.scalar_tensor_tensor(
+                    out=dg[:],
+                    in0=stt[:, i * P : (i + 1) * P],
+                    scalar=1.0,
+                    in1=ident[:],
+                    op0=ALU.mult,
+                    op1=ALU.mult,
+                    accum_out=s["ssq"][:, NS + i : NS + i + 1],
+                )
             nc.vector.tensor_tensor(out=s["dd"][:], in0=s["cpiv"][:], in1=s["mean"][:], op=ALU.subtract)
             nc.vector.tensor_tensor(out=s["d2"][:], in0=s["dd"][:], in1=s["dd"][:], op=ALU.mult)
 
@@ -291,7 +298,7 @@ def tile_decoder_pb_t_kernel(tc, h7_pre, g7, be7, W8, b8, out):
         def d1(w, k0=0, k1=KT):
             s = st[w // NH]
             r = rt[w]
-            for kt in range(k0, k1):
+            for kt in [k for k in range(k0, k1) if k >= 4] + [k for k in range(k0, k1) if k < 4]:
                 nc.vector.tensor_scalar(
                     out=r[:, kt, :],
                     in0=r[:, kt, :],
@@ -357,7 +364,7 @@ def tile_decoder_pb_t_kernel(tc, h7_pre, g7, be7, W8, b8, out):
 
         def store(w, j0, j1):
             u = w % NH
-            nc.scalar.dma_start(out=ov[w // NH][:, 4 * u + j0 : 4 * u + j1, :], in_=yt[w][:, j0:j1, :])
+            nc.sync.dma_start(out=ov[w // NH][:, 4 * u + j0 : 4 * u + j1, :], in_=yt[w][:, j0:j1, :])
 
         def who(w, g):
             if w < 2:
@@ -396,6 +403,10 @@ def tile_decoder_pb_t_kernel(tc, h7_pre, g7, be7, W8, b8, out):
             quant(w)
             if w == NH:
                 w_q(1)
+            if w + 1 < NU:
+                for g in range(2):
+                    if who(w + 1, g) == "V":
+                        d2(w + 1, g, "V")
             if u == NH - 1:
                 d1(u, 0, 4)
                 d2(u, 0, "G")
@@ -427,10 +438,6 @@ def tile_decoder_pb_t_kernel(tc, h7_pre, g7, be7, W8, b8, out):
                 for g in range(2):
                     if who(u, g) == "S":
                         d2(u, g, "S")
-            if w + 1 < NU:
-                for g in range(2):
-                    if who(w + 1, g) == "V":
-                        d2(w + 1, g, "V")
             if nxt < NU:
                 p1(nxt)
             nxt += 1

@@ -27,6 +27,7 @@ NS = KT - NG
 PRE = 2
 SUMCOL = 384
 BF16_MAX = 3.3895313892515355e38
+GC = 448
 FLOPS = 2 * NB * N * K * C
 
 
@@ -312,9 +313,10 @@ def tile_decoder_pb_t_kernel(tc, h7_pre, g7, be7, W8, b8, out):
             if w not in grp:
                 grp[w] = gpool.tile([P, 2, 512, 4], BF16, name="grp", align_bytes=64)
             if eng == "G":
+                gc = GC if w > NH + 1 else 512
                 nc.gpsimd.tensor_scalar(
-                    out=grp[w][:, g],
-                    in0=rt[w][:, 4 * g : 4 * g + 4, :].rearrange("p t c -> p c t"),
+                    out=grp[w][:, g, 0:gc, :],
+                    in0=rt[w][:, 4 * g : 4 * g + 4, 0:gc].rearrange("p t c -> p c t"),
                     scalar1=BF16_MAX,
                     scalar2=0.0,
                     op0=ALU.min,
@@ -438,6 +440,12 @@ def tile_decoder_pb_t_kernel(tc, h7_pre, g7, be7, W8, b8, out):
                 for g in range(2):
                     if who(u, g) == "S":
                         d2(u, g, "S")
+                if u > NH + 1:
+                    nc.scalar.activation(
+                        out=grp[u][:, 0, GC:512, :].rearrange("p (c i) t -> p c t i", i=4),
+                        in_=rt[u][:, 0:4, GC:512].rearrange("p t (c i) -> p c t i", i=4),
+                        func=ACT.Relu,
+                    )
             if nxt < NU:
                 p1(nxt)
             nxt += 1

from contextlib import ExitStack

import concourse.mybir as mybir
from concourse.masks import make_identity

F32 = mybir.dt.float32
BF16 = mybir.dt.bfloat16
U32 = mybir.dt.uint32
U8 = mybir.dt.uint8
FP8X4 = mybir.dt.float8_e4m3fn_x4
ALU = mybir.AluOpType
ACT = mybir.ActivationFunctionType
AX = mybir.AxisListType

P = 128
NB = 2
N = 4096
K = 1024
C = 512
EPS = 1e-5
NJ = N // P
KT = K // P
NH = 8
NU = NB * NH
NG = 3
NS = KT - NG
PRE = 2
SUMCOL = 384
BF16_MAX = 3.3895313892515355e38
GC = 448
FLOPS = 2 * NB * N * K * C


def tile_decoder_pb_t_kernel(tc, h7_pre, g7, be7, W8, b8, out):
    nc = tc.nc
    with ExitStack() as ctx:
        ctx.enter_context(tc.manual_schedule())
        keep = ctx.enter_context(tc.tile_pool(name="keep", bufs=1))
        xpool = ctx.enter_context(tc.tile_pool(name="xpool", bufs=5))
        rtpool = ctx.enter_context(tc.tile_pool(name="rtpool", bufs=13))
        gpool = ctx.enter_context(tc.tile_pool(name="gpool", bufs=3))
        cpool = ctx.enter_context(tc.tile_pool(name="cpool", bufs=3))
        ypool = ctx.enter_context(tc.tile_pool(name="ypool", bufs=3))
        jpool = ctx.enter_context(tc.tile_pool(name="jpool", bufs=2))
        dpool = ctx.enter_context(tc.tile_pool(name="dpool", bufs=2))
        tpool = ctx.enter_context(tc.psum_pool(name="tpool", bufs=3))
        apool = ctx.enter_context(tc.psum_pool(name="apool", bufs=4))
        spool = ctx.enter_context(tc.psum_pool(name="spool", bufs=1))

        xv = [h7_pre[b].rearrange("(p j) k -> p j k", j=NJ) for b in range(NB)]
        ov = [out[:, b, :].rearrange("(p j) c -> p j c", j=NJ) for b in range(NB)]

        xt = {}
        tps = {}
        rt = {}
        grp = {}
        codes = {}
        acc = {}
        yt = {}
        wn = {}
        gws = {}
        wc = {}
        ws = {}
        bias = {}
        st = {}
        state = {"ld": 0}

        ident = keep.tile([P, P], BF16, name="ident")
        make_identity(nc, ident[:])
        ones = keep.tile([P, 2], BF16, name="ones")
        nc.vector.memset(ones[:], 1.0)
        mhalf = keep.tile([P, KT], F32, name="mhalf")
        nc.vector.memset(mhalf[:], -0.5)
        warm = keep.tile([P, 1], F32, name="warm")
        nc.vector.memset(warm[:], 0.0)
        nc.scalar.activation(out=warm[:], in_=warm[:], func=ACT.Sigmoid)
        gbrows = keep.tile([P, P], BF16, name="gbrows")
        nc.vector.memset(gbrows[:], 0.0)
        gb = keep.tile([P, 4 * KT], F32, name="gb")
        stt = spool.tile([P, 512], F32, name="stt")
        for b in range(NB):
            st[b] = {
                "sq": keep.tile([P, NS, NH], F32, name="sq%d" % b),
                "cpiv": keep.tile([P, KT], F32, name="cpiv%d" % b),
            }
            nc.vector.memset(st[b]["cpiv"][:], 0.0)
        st[0]["sm"] = keep.tile([P, KT, NH], F32, name="sm0")

        def load_w(b):
            wn[b] = rtpool.tile([P, 4, K], BF16, name="wn", tag="rt", align_bytes=64)
            nc.sync.dma_start(out=wn[b][:], in_=W8[b].rearrange("(a p) k -> p a k", p=P))

        def load_gb():
            nc.sync.dma_start(out=gbrows[0:16, :], in_=g7.rearrange("b (t p) -> (b t) p", p=P))
            nc.sync.dma_start(out=gbrows[16:32, :], in_=be7.rearrange("b (t p) -> (b t) p", p=P))

        def load_bias():
            for b in range(NB):
                bias[b] = keep.tile([P, C], BF16, name="bias%d" % b)
                nc.sync.dma_start(out=bias[b][:], in_=b8[b].partition_broadcast(P))

        def load_x():
            a = state["ld"]
            if a < NU:
                xt[a] = xpool.tile([P, 4, K], BF16, name="xt")
                src = xv[a // NH][:, 4 * (a % NH) : 4 * (a % NH) + 4, :]
                if a == 0:
                    for q in range(4):
                        nc.sync.dma_start(out=xt[a][:, :, 256 * q : 256 * (q + 1)], in_=src[:, :, 256 * q : 256 * (q + 1)])
                else:
                    nc.sync.dma_start(out=xt[a][:], in_=src)
                state["ld"] = a + 1
                if a == 7:
                    load_gb()
                    load_w(0)
                if a == 9:
                    load_bias()
                if a == 11:
                    load_w(1)

        def w_tr(b, part):
            if part == 0:
                gws[b] = rtpool.tile([P, 2, C, 4], BF16, name="gw", tag="rt", align_bytes=64)
            gw = gws[b]
            g = part // 2
            hc = part % 2
            tp = tpool.tile([P, 1024], BF16, name="tp")
            for t in range(4):
                for a in range(2):
                    nc.tensor.transpose(
                        tp[:, t * 256 + a * P : t * 256 + (a + 1) * P],
                        wn[b][:, 2 * hc + a, (4 * g + t) * P : (4 * g + t + 1) * P],
                        ident[:],
                    )
            dst = gw[:, g, hc * 256 : (hc + 1) * 256, :]
            src = tp[:].rearrange("p (t c) -> p c t", t=4)
            nc.scalar.copy(out=dst, in_=src)

        def w_q(b):
            gw = gws[b]
            wc[b] = keep.tile([P, 2, C], U32, name="wc%d" % b, align_bytes=64)
            ws[b] = keep.tile([P, 2, C], U8, name="ws%d" % b, align_bytes=64)
            nc.vector.quantize_mx(
                out=wc[b][:].rearrange("p g c -> p (g c)").bitcast(FP8X4),
                scales=ws[b][:].rearrange("p g c -> p (g c)"),
                in_=gw[:].rearrange("p g c t -> p (g c t)"),
            )

        def prep_gb():
            tp = tpool.tile([P, 1024], BF16, name="tp")
            nc.tensor.transpose(tp[:, 0:P], gbrows[:], ident[:])
            nc.vector.tensor_copy(out=gb[:], in_=tp[:, 0 : 4 * KT])

        def gram(a):
            b = a // NH
            h = a % NH
            x = xt[a]
            for i in range(NG):
                for jj in range(4):
                    nc.tensor.matmul(
                        out=stt[:, i * P : (i + 1) * P],
                        lhsT=x[:, jj, (NS + i) * P : (NS + i + 1) * P],
                        rhs=x[:, jj, (NS + i) * P : (NS + i + 1) * P],
                        start=(h == 0 and i == 0 and jj == 0),
                        stop=(b == 0 and h == NH - 1 and i == NG - 1 and jj == 3),
                    )

        def sums(a):
            h = a % NH
            x = xt[a]
            for jj in range(4):
                for kt in range(KT):
                    nc.tensor.matmul(
                        out=stt[:, SUMCOL + kt : SUMCOL + kt + 1],
                        lhsT=x[:, jj, kt * P : (kt + 1) * P],
                        rhs=ones[:, 0:1],
                        start=False,
                        stop=(h == NH - 1 and jj == 3 and kt == KT - 1),
                    )

        def flip(a, q, nk=2):
            x = xt[a]
            tp = tpool.tile([P, 1024], BF16, name="tp")
            tps[(a, q)] = tp
            for k2 in range(nk):
                for jj in range(4):
                    nc.tensor.transpose(
                        tp[:, k2 * 512 + jj * P : k2 * 512 + (jj + 1) * P],
                        x[:, jj, (2 * q + k2) * P : (2 * q + k2 + 1) * P],
                        ident[:],
                    )

        def square(a, kt, src):
            s = st[a // NH]
            junk = jpool.tile([P, 512], BF16, name="junk")
            nc.scalar.activation(
                out=junk[:],
                in_=src,
                func=ACT.Square,
                bias=s["cpiv"][:, kt : kt + 1],
                scale=-1.0,
                accum_out=s["sq"][:, kt, a % NH : a % NH + 1],
            )

        def p1_head(a):
            s = st[0]
            r = rtpool.tile([P, KT, 512], BF16, name="rt", tag="rt", align_bytes=64)
            rt[a] = r
            for q in range(4):
                if q == 3:
                    gram(a)
                flip(a, q)
                for k2 in range(2):
                    nc.vector.tensor_scalar(
                        out=r[:, 2 * q + k2, :],
                        in0=tps[(a, q)][:, k2 * 512 : (k2 + 1) * 512],
                        scalar1=1.0,
                        scalar2=0.0,
                        op0=ALU.mult,
                        op1=ALU.add,
                        accum_out=s["sm"][:, 2 * q + k2, a : a + 1],
                    )
                if a == 0 and q == 2:
                    nc.vector.tensor_copy(out=s["cpiv"][:, 0:NS], in_=r[:, 0:NS, 0])
            load_x()
            for kt in range(NS):
                square(a, kt, r[:, kt, :])

        def bank_out(a, q, eng):
            dst = rt[a][:, 2 * q : 2 * q + 2, :]
            src = tps[(a, q)][:].rearrange("p (k n) -> p k n", k=2)
            if eng == "V":
                nc.vector.tensor_copy(out=dst, in_=src)
            else:
                nc.scalar.copy(out=dst, in_=src)

        def p1(a):
            s = st[1]
            rt[a] = rtpool.tile([P, KT, 512], BF16, name="rt", tag="rt", align_bytes=64)
            for q in range(3):
                flip(a, q)
            bank_out(a, 0, "S")
            flip(a, 3)
            gram(a)
            sums(a)
            bank_out(a, 1, "S")
            nc.scalar.copy(out=rt[a][:, 4, :], in_=tps[(a, 2)][:, 0:512])
            if a == NH:
                nc.scalar.copy(out=s["cpiv"][:, 0:NS], in_=rt[a][:, 0:NS, 0])
            load_x()
            for kt in range(NS):
                square(a, kt, rt[a][:, kt, :])

        def p1_v(a):
            nc.vector.tensor_copy(out=rt[a][:, 5, :], in_=tps[(a, 2)][:, 512:1024])
            bank_out(a, 3, "V")

        def fin_mean(b):
            s = st[b]
            for nm in ("mean", "dd", "d2", "ssq", "var", "ve", "rstd", "sc", "ms", "sh"):
                s[nm] = keep.tile([P, KT], F32, name="%s%d" % (nm, b))
            if b == 0:
                s["tot"] = keep.tile([P, KT], F32, name="tot%d" % b)
                nc.vector.tensor_reduce(out=s["tot"][:], in_=s["sm"][:], axis=AX.X, op=ALU.add)
                nc.vector.tensor_scalar(out=s["mean"][:], in0=s["tot"][:], scalar1=1.0 / N, scalar2=None, op0=ALU.mult)
            else:
                nc.vector.tensor_scalar(
                    out=s["mean"][:], in0=stt[:, SUMCOL : SUMCOL + KT], scalar1=1.0 / N, scalar2=None, op0=ALU.mult
                )
            for i in range(NG):
                dg = dpool.tile([P, P], F32, name="dg")
                nc.vector.scalar_tensor_tensor(
                    out=dg[:],
                    in0=stt[:, i * P : (i + 1) * P],
                    scalar=1.0,
                    in1=ident[:],
                    op0=ALU.mult,
                    op1=ALU.mult,
                    accum_out=s["ssq"][:, NS + i : NS + i + 1],
                )
            nc.vector.tensor_tensor(out=s["dd"][:], in0=s["cpiv"][:], in1=s["mean"][:], op=ALU.subtract)
            nc.vector.tensor_tensor(out=s["d2"][:], in0=s["dd"][:], in1=s["dd"][:], op=ALU.mult)

        def fin_a(b):
            s = st[b]
            nc.vector.tensor_reduce(out=s["ssq"][:, 0:NS], in_=s["sq"][:], axis=AX.X, op=ALU.add)
            nc.vector.scalar_tensor_tensor(
                out=s["var"][:], in0=s["ssq"][:], scalar=1.0 / N, in1=s["d2"][:], op0=ALU.mult, op1=ALU.subtract
            )
            nc.vector.tensor_scalar(out=s["ve"][:], in0=s["var"][:], scalar1=0.0, scalar2=EPS, op0=ALU.max, op1=ALU.add)
            nc.gpsimd.tensor_tensor(out=s["rstd"][:], in0=s["ve"][:], in1=mhalf[:], op=ALU.pow)

        def fin_b(b):
            s = st[b]
            nc.vector.tensor_tensor(out=s["sc"][:], in0=gb[:, b * KT : (b + 1) * KT], in1=s["rstd"][:], op=ALU.mult)
            nc.vector.tensor_tensor(out=s["ms"][:], in0=s["mean"][:], in1=s["sc"][:], op=ALU.mult)
            nc.vector.tensor_tensor(out=s["sh"][:], in0=gb[:, (2 + b) * KT : (3 + b) * KT], in1=s["ms"][:], op=ALU.subtract)

        def d1(w, k0=0, k1=KT):
            s = st[w // NH]
            r = rt[w]
            for kt in [k for k in range(k0, k1) if k >= 4] + [k for k in range(k0, k1) if k < 4]:
                nc.vector.tensor_scalar(
                    out=r[:, kt, :],
                    in0=r[:, kt, :],
                    scalar1=s["sc"][:, kt : kt + 1],
                    scalar2=s["sh"][:, kt : kt + 1],
                    op0=ALU.mult,
                    op1=ALU.add,
                )

        def d2(w, g, eng):
            if w not in grp:
                grp[w] = gpool.tile([P, 2, 512, 4], BF16, name="grp", align_bytes=64)
            if eng == "G":
                gc = GC if w > NH + 1 else 512
                nc.gpsimd.tensor_scalar(
                    out=grp[w][:, g, 0:gc, :],
                    in0=rt[w][:, 4 * g : 4 * g + 4, 0:gc].rearrange("p t c -> p c t"),
                    scalar1=BF16_MAX,
                    scalar2=0.0,
                    op0=ALU.min,
                    op1=ALU.max,
                )
                return
            dst = grp[w][:, g].rearrange("p (c i) t -> p c t i", i=4)
            src = rt[w][:, 4 * g : 4 * g + 4, :].rearrange("p t (c i) -> p c t i", i=4)
            if eng == "S":
                nc.scalar.activation(out=dst, in_=src, func=ACT.Relu)
            else:
                nc.vector.tensor_scalar(out=dst, in0=src, scalar1=0.0, scalar2=None, op0=ALU.max)

        def quant(w):
            ac = cpool.tile([P, 2, 512], U32, name="ac", align_bytes=64)
            asc = cpool.tile([P, 2, 512], U8, name="asc", align_bytes=64)
            codes[w] = (ac, asc)
            nc.vector.quantize_mx(
                out=ac[:].rearrange("p g c -> p (g c)").bitcast(FP8X4),
                scales=asc[:].rearrange("p g c -> p (g c)"),
                in_=grp[w][:].rearrange("p g c t -> p (g c t)"),
            )

        def mx(w, jj):
            b = w // NH
            ac, asc = codes[w]
            t = apool.tile([P, C], F32, name="acc")
            acc[(w, jj)] = t
            for g in range(2):
                nc.tensor.matmul_mx(
                    out=t[:],
                    lhsT=ac[:, g, jj * P : (jj + 1) * P].bitcast(FP8X4),
                    lhsT_scale=asc[:, g, jj * P : (jj + 1) * P],
                    rhs=wc[b][:, g, :].bitcast(FP8X4),
                    rhs_scale=ws[b][:, g, :],
                    start=(g == 0),
                    stop=(g == 1),
                )

        def addb(w, jj):
            if jj == 0:
                yt[w] = ypool.tile([P, 4, C], F32, name="y")
            nc.vector.tensor_tensor(out=yt[w][:, jj, :], in0=acc[(w, jj)][:], in1=bias[w // NH][:], op=ALU.add)

        def sigm(w, j0, j1):
            nc.scalar.activation(out=yt[w][:, j0:j1, :], in_=yt[w][:, j0:j1, :], func=ACT.Sigmoid)

        def store(w, j0, j1):
            u = w % NH
            nc.sync.dma_start(out=ov[w // NH][:, 4 * u + j0 : 4 * u + j1, :], in_=yt[w][:, j0:j1, :])

        def who(w, g):
            if w < 2:
                return "V"
            if w == 2:
                return "S" if g == 0 else "V"
            if w == NH - 1:
                return "G"
            if w == NH:
                return "S" if g == 0 else "V"
            if g == 0:
                return "G"
            return "V" if w <= NH + 1 else "S"

        for i in range(5):
            load_x()
        for a in range(NH):
            p1_head(a)
        prep_gb()
        for part in range(4):
            w_tr(0, part)
        fin_mean(0)
        fin_a(0)
        fin_b(0)
        d1(0)
        d2(0, 0, "V")
        d2(0, 1, "V")
        w_q(0)
        p1(NH)
        p1_v(NH)
        d1(1)
        p1(NH + 1)
        nxt = NH + PRE
        for w in range(NU):
            u = w + 2
            quant(w)
            if w == NH:
                w_q(1)
            if w + 1 < NU:
                for g in range(2):
                    if who(w + 1, g) == "V":
                        d2(w + 1, g, "V")
            if u == NH - 1:
                d1(u, 0, 4)
                d2(u, 0, "G")
            elif u == NH:
                d1(u - 1, 4, KT)
                d2(u - 1, 1, "G")
            elif u < NU:
                d1(u)
                if who(u, 0) == "G":
                    d2(u, 0, "G")
            for jj in range(4):
                if w > 0:
                    addb(w - 1, jj)
                mx(w, jj)
                if w > 0 and jj % 2 == 1:
                    sigm(w - 1, jj - 1, jj + 1)
            if w > 0:
                store(w - 1, 0, 4)
            if nxt - 1 < NU and w <= NH - 2:
                p1_v(nxt - 1)
            if w == NH - 2:
                for part in range(4):
                    w_tr(1, part)
                fin_mean(1)
                fin_a(1)
                fin_b(1)
                d1(NH)
            if u < NU:
                for g in range(2):
                    if who(u, g) == "S":
                        d2(u, g, "S")
                if u > NH + 1:
                    nc.scalar.activation(
                        out=grp[u][:, 0, GC:512, :].rearrange("p (c i) t -> p c t i", i=4),
                        in_=rt[u][:, 0:4, GC:512].rearrange("p t (c i) -> p c t i", i=4),
                        func=ACT.Relu,
                    )
            if nxt < NU:
                p1(nxt)
            nxt += 1
        last = NU - 1
        for jj in range(4):
            addb(last, jj)
            sigm(last, jj, jj + 1)
            if jj % 2 == 1:
                store(last, jj - 1, jj + 1)
